import numpy as np
import ml_dtypes


def mxq(x, axis, fmt="e4m3"):
    dtype, down = {"e4m3": (ml_dtypes.float8_e4m3fn, 7), "e5m2": (ml_dtypes.float8_e5m2, 14)}[fmt]
    v = np.moveaxis(np.asarray(x, np.float32).astype(ml_dtypes.bfloat16).astype(np.float64), axis, -1)
    blocks = v.reshape(v.shape[:-1] + (-1, 32))
    amax = np.abs(blocks).max(-1, keepdims=True)
    byte = np.maximum(np.where(amax > 0, np.frexp(amax)[1] - 1 + 127, 0) - down, 1)
    scale = np.exp2(byte - 127.0)
    codes = (blocks / scale).astype(np.float32).astype(dtype).astype(np.float64)
    return np.moveaxis((codes * scale).reshape(v.shape), -1, axis)


WIDE = False


def mx_kscale(k):
    if not WIDE:
        return np.ones(k)
    levels = np.array([10, -10, 5, -5, 0])
    a = np.random.permutation(np.resize(levels, k // 512 * 4)).reshape(k // 512, 4)
    idx = np.arange(k)
    return np.exp2(a[idx // 512, idx % 128 // 32])


BF16 = ml_dtypes.bfloat16


def bf(x):
    return np.asarray(x, np.float32).astype(BF16)


def f64(x):
    return np.asarray(x).astype(np.float64)


M, K, N = 1024, 2048, 2048

EPS = 1e-08


def setup_inputs():
    limit = np.sqrt(6.0 / (K + N))
    s = mx_kscale(K)
    g = np.exp2(np.round(np.log2(s.max() / s.min()) / 4))
    return {"x": bf(np.random.standard_normal((M, K)) * s[None, :]),
            "weight": bf(np.random.uniform(-limit, limit, (N, K)) / s[None, :] * g),
            "mask": bf((np.random.random((N, K)) < 0.8).astype(np.float64)),
            "bias": bf(np.random.standard_normal(N) * 0.1)}


def reference(x, weight, mask, bias):
    mw = f64(weight) * f64(mask)
    aw = np.abs(mw)
    scale = aw.mean() + EPS
    threshold = np.std(aw, ddof=1) * 0.5
    tern = np.where(mw > threshold, 1.0, 0.0) + np.where(mw < -threshold, -1.0, 0.0)
    tw = tern * scale
    return (mxq(f64(x), 1, "e4m3") @ mxq(tw, 1, "e4m3").T) + f64(bias)

@@ -1,0 +1,205 @@
+from contextlib import ExitStack
+
+import concourse.mybir as mybir
+from concourse.masks import make_identity
+
+FLOPS = 2 * 1024 * 2048 * 2048
+
+F32 = mybir.dt.float32
+BF16 = mybir.dt.bfloat16
+I32 = mybir.dt.int32
+U32 = mybir.dt.uint32
+U8 = mybir.dt.uint8
+FP8X4 = mybir.dt.float8_e4m3fn_x4
+ALU = mybir.AluOpType
+ACT = mybir.ActivationFunctionType
+
+P = 128
+M, K, N = 1024, 2048, 2048
+G = K // 512
+ROWS = 256
+W_LOADS = N // ROWS
+X_LOADS = M // ROWS
+PIECE = G * ROWS * 4
+COUNT = N * K
+DIAG_BLOCKS = 10
+SQ_COLS = K - DIAG_BLOCKS * P
+ONES_N = 8
+
+
+def tile_masklockedlinear_kernel(tc, x, weight, mask, bias, out):
+    nc = tc.nc
+    with ExitStack() as ctx:
+        const = ctx.enter_context(tc.tile_pool(name="const", bufs=1))
+        stream = ctx.enter_context(tc.tile_pool(name="stream", bufs=3))
+        big = ctx.enter_context(tc.tile_pool(name="big", bufs=W_LOADS))
+        psum = ctx.enter_context(tc.psum_pool(name="psum", bufs=1))
+
+        def bank(i, shape):
+            return psum.tile(shape, F32, name="bank%d" % i, tag="bank%d" % i)
+
+        brow = const.tile([P, N], BF16, name="brow")
+        nc.vector.memset(brow[:], 0.0)
+        nc.sync.dma_start(out=brow[0:1, :], in_=bias.rearrange("(o n) -> o n", o=1))
+        ident = const.tile([P, P], F32, name="ident")
+        make_identity(nc, ident[:])
+        mean_w = const.tile([P, P], F32, name="mean_w")
+        nc.vector.memset(mean_w[:], 1.0 / COUNT)
+        ones_b = const.tile([P, P], BF16, name="ones_b")
+        nc.vector.memset(ones_b[:], 1.0)
+        warm = const.tile([P, 1], F32, name="warm")
+        nc.scalar.activation(out=warm[:], in_=mean_w[:, 0:1], func=ACT.Sqrt)
+
+        w_view = weight.rearrange("(a p r) k -> a p (r k)", p=P, r=2)
+        m_view = mask.rearrange("(a p r) k -> a p (r k)", p=P, r=2)
+        x_view = x.rearrange("(a p r) k -> a p (r k)", p=P, r=2)
+        o_view = out.rearrange("(i p) n -> p i n", p=P)
+
+        def transpose_rows(src, dst):
+            words = src.bitcast(F32)
+            dwords = dst.bitcast(F32)
+            for g in range(G):
+                pt = bank(g, [P, 512])
+                for r in range(2):
+                    for u in range(2):
+                        col = r * 1024 + 256 * g + 128 * u
+                        nc.tensor.transpose(pt[:, (2 * r + u) * P:(2 * r + u + 1) * P], words[:, col:col + P], ident[:])
+                nc.scalar.copy(
+                    out=dwords[:, g * 512:(g + 1) * 512].rearrange("p (j r u) -> p j r u", r=2, u=2),
+                    in_=pt[:].rearrange("p (r u j) -> p j r u", r=2, u=2),
+                )
+
+        bias_bc = const.tile([P, N], BF16, name="bias_bc")
+        for c in range(4):
+            pb = bank(4 + c, [P, 512])
+            nc.tensor.matmul(pb[:], lhsT=ones_b[:], rhs=brow[:, c * 512:(c + 1) * 512], start=True, stop=True)
+            nc.scalar.copy(out=bias_bc[:, c * 512:(c + 1) * 512], in_=pb[:])
+
+        acc_a = bank(4, [P, ONES_N])
+        acc_d = bank(5, [P, P])
+        sacc = const.tile([P, 2 * W_LOADS], F32, name="sacc")
+        aw = []
+        sg = []
+        n_a = W_LOADS * 32
+        n_d = W_LOADS * 2 * DIAG_BLOCKS
+
+        def stage1(a):
+            wt = stream.tile([P, 2 * K], BF16, name="wt", tag="w", bufs=4)
+            mk = stream.tile([P, 2 * K], BF16, name="mk", tag="m", align_bytes=64)
+            nc.sync.dma_start(out=wt[:], in_=w_view[a])
+            nc.sync.dma_start(out=mk[:], in_=m_view[a])
+            for r in range(2):
+                sl = slice(r * K, (r + 1) * K)
+                nc.vector.tensor_tensor(out=wt[:, sl], in0=wt[:, sl], in1=mk[:, sl], op=ALU.mult)
+            aw.append(big.tile([P, PIECE], BF16, name="aw%d" % a, tag="aw", align_bytes=64))
+            sg.append(big.tile([P, PIECE], BF16, name="sg%d" % a, tag="sg", align_bytes=64))
+            transpose_rows(wt[:], sg[a][:])
+            for r in range(2):
+                for b in range(DIAG_BLOCKS):
+                    i_d = (a * 2 + r) * DIAG_BLOCKS + b
+                    blk = wt[:, r * K + b * P:r * K + (b + 1) * P]
+                    nc.tensor.matmul(acc_d[:], lhsT=blk, rhs=blk, start=(i_d == 0), stop=(i_d == n_d - 1))
+                junk = stream.tile([P, SQ_COLS], BF16, name="junk", tag="junk", bufs=2)
+                nc.scalar.activation(
+                    out=junk[:], in_=wt[:, r * K + DIAG_BLOCKS * P:(r + 1) * K], func=ACT.Square,
+                    accum_out=sacc[:, 2 * a + r:2 * a + r + 1],
+                )
+
+        def stage2(a):
+            nc.vector.tensor_single_scalar(out=aw[a][:].bitcast(I32), in_=sg[a][:].bitcast(I32), scalar=0x7FFF7FFF, op=ALU.bitwise_and)
+            nc.vector.tensor_scalar(out=sg[a][:], in0=sg[a][:], scalar1=0.0, scalar2=0.5, op0=ALU.is_ge, op1=ALU.subtract)
+            for q in range(32):
+                i_a = a * 32 + q
+                nc.tensor.matmul(acc_a[:], lhsT=aw[a][:, q * P:(q + 1) * P], rhs=ones_b[:, 0:ONES_N], start=(i_a == 0), stop=(i_a == n_a - 1))
+
+        for a in range(W_LOADS):
+            stage1(a)
+            if a >= 1:
+                stage2(a - 1)
+        stage2(W_LOADS - 1)
+
+        zt = const.tile([P, 2 + P], F32, name="zt")
+        nc.vector.tensor_copy(out=zt[:, 0:2], in_=acc_a[:, 0:2])
+        nc.vector.tensor_tensor(out=zt[:, 2:2 + P], in0=acc_d[:], in1=ident[:], op=ALU.mult)
+        tot = bank(6, [P, 2 + P + 2 * W_LOADS])
+        nc.tensor.matmul(tot[:, 2 + P:], lhsT=mean_w[:], rhs=sacc[:], start=True, stop=True)
+        nc.tensor.matmul(tot[:, 0:2 + P], lhsT=mean_w[:], rhs=zt[:], start=True, stop=True)
+        st = const.tile([P, 8], F32, name="st")
+        nc.vector.tensor_reduce(out=st[:, 0:1], in_=tot[:, 2:], axis=mybir.AxisListType.X, op=ALU.add)
+        nc.vector.tensor_copy(out=st[:, 1:2], in_=tot[:, 0:1])
+        nc.vector.scalar_tensor_tensor(out=st[:, 2:3], in0=st[:, 1:2], scalar=st[:, 1:2], in1=st[:, 0:1], op0=ALU.mult, op1=ALU.subtract)
+        nc.vector.tensor_scalar(out=st[:, 3:4], in0=st[:, 2:3], scalar1=-0.25 * COUNT / (COUNT - 1), scalar2=0.0, op0=ALU.mult, op1=ALU.max)
+        thr = const.tile([P, 1], F32, name="thr")
+        nc.scalar.activation(out=thr[:], in_=st[:, 3:4], func=ACT.Sqrt)
+        nc.vector.tensor_scalar(out=st[:, 4:5], in0=st[:, 1:2], scalar1=2.0, scalar2=2e-8, op0=ALU.mult, op1=ALU.add)
+
+        xc = const.tile([P, X_LOADS * G * ROWS], U32, name="xc", align_bytes=64)
+        xs = const.tile([P, X_LOADS * G * ROWS], U8, name="xs", align_bytes=64)
+
+        def load_x(b):
+            xt = stream.tile([P, 2 * K], BF16, name="xt", tag="w", bufs=4)
+            nc.sync.dma_start(out=xt[:], in_=x_view[b])
+            xg = stream.tile([P, PIECE], BF16, name="xg", tag="m", align_bytes=64)
+            transpose_rows(xt[:], xg[:])
+            sl = slice(b * G * ROWS, (b + 1) * G * ROWS)
+            nc.vector.quantize_mx(out=xc[:, sl].bitcast(FP8X4), scales=xs[:, sl], in_=xg[:])
+
+        wc = []
+        ws = []
+        accs = []
+
+        def prepare(i):
+            if i == 0:
+                wc.append(const.tile([P, G * ROWS], U32, name="wc0", align_bytes=64))
+                ws.append(const.tile([P, G * ROWS], U8, name="ws0", align_bytes=64))
+            else:
+                wc.append(big.tile([P, G * ROWS], U32, name="wc%d" % i, tag="aw", align_bytes=64))
+                ws.append(big.tile([P, G * ROWS], U8, name="ws%d" % i, tag="sg", align_bytes=64))
+            nc.vector.tensor_scalar(out=aw[i][:], in0=aw[i][:], scalar1=thr[:, 0:1], scalar2=st[:, 4:5], op0=ALU.is_gt, op1=ALU.mult)
+            nc.vector.tensor_tensor(out=sg[i][:], in0=aw[i][:], in1=sg[i][:], op=ALU.mult)
+            nc.vector.quantize_mx(out=wc[i][:].bitcast(FP8X4), scales=ws[i][:], in_=sg[i][:])
+
+        def multiply(i):
+            mine = []
+            for b in range(X_LOADS):
+                acc = bank(((i + 1) % 2) * 4 + b, [P, 2 * ROWS])
+                for h in range(2):
+                    for g in range(G):
+                        lo = b * G * ROWS + g * ROWS + h * P
+                        nc.tensor.matmul_mx(
+                            out=acc[:, h * ROWS:(h + 1) * ROWS],
+                            lhsT=xc[:, lo:lo + P].bitcast(FP8X4), lhsT_scale=xs[:, lo:lo + P],
+                            rhs=wc[i][:, g * ROWS:(g + 1) * ROWS].bitcast(FP8X4), rhs_scale=ws[i][:, g * ROWS:(g + 1) * ROWS],
+                            start=(g == 0), stop=(g == G - 1),
+                        )
+                mine.append(acc)
+            accs.append(mine)
+
+        def finish(i):
+            ot = stream.tile([P, 8 * ROWS], F32, name="ot", tag="w", bufs=4)
+            cols = slice(i * ROWS, (i + 1) * ROWS)
+            for b in range(X_LOADS):
+                nc.vector.tensor_tensor(
+                    out=ot[:, b * 2 * ROWS:(b + 1) * 2 * ROWS].rearrange("p (h n) -> p h n", h=2),
+                    in0=accs[i][b][:].rearrange("p (h n) -> p h n", h=2),
+                    in1=bias_bc[:, cols].unsqueeze(1).to_broadcast([P, 2, ROWS]),
+                    op=ALU.add,
+                )
+                if b % 2 == 1:
+                    nc.sync.dma_start(
+                        out=o_view[:, (b - 1) * 2:(b + 1) * 2, cols],
+                        in_=ot[:, (b - 1) * 2 * ROWS:(b + 1) * 2 * ROWS].rearrange("p (i n) -> p i n", i=4),
+                    )
+
+        prepare(0)
+        for b in range(X_LOADS):
+            load_x(b)
+        multiply(0)
+        prepare(1)
+        multiply(1)
+        for i in range(2, W_LOADS):
+            finish(i - 2)
+            prepare(i)
+            multiply(i)
+        finish(W_LOADS - 2)
+        finish(W_LOADS - 1)

@@ -22,9 +22,11 @@ W_LOADS = N // ROWS
 X_LOADS = M // ROWS
 PIECE = G * ROWS * 4
 COUNT = N * K
-DIAG_BLOCKS = 10
-SQ_COLS = K - DIAG_BLOCKS * P
-ONES_N = 8
+DIAG_BLOCKS = [10, 10, 10, 10, 10, 10, 10, 16]
+ONES_N = 2
+KINDS = "TNTTNTTN"
+SPLIT = [0, W_LOADS - 1]
+LATE_SIGN = 3
 
 
 def tile_masklockedlinear_kernel(tc, x, weight, mask, bias, out):
@@ -41,6 +43,9 @@ def tile_masklockedlinear_kernel(tc, x, weight, mask, bias, out):
         brow = const.tile([P, N], BF16, name="brow")
         nc.vector.memset(brow[:], 0.0)
         nc.sync.dma_start(out=brow[0:1, :], in_=bias.rearrange("(o n) -> o n", o=1))
+        bsq_b = const.tile([P, P], BF16, name="bsq_b")
+        nc.vector.memset(bsq_b[:], 0.0)
+        nc.sync.dma_start(out=bsq_b[0:N // P, :], in_=bias.rearrange("(t n) -> t n", n=P))
         ident = const.tile([P, P], F32, name="ident")
         make_identity(nc, ident[:])
         mean_w = const.tile([P, P], F32, name="mean_w")
@@ -50,103 +55,141 @@ def tile_masklockedlinear_kernel(tc, x, weight, mask, bias, out):
         warm = const.tile([P, 1], F32, name="warm")
         nc.scalar.activation(out=warm[:], in_=mean_w[:, 0:1], func=ACT.Sqrt)
 
-        w_view = weight.rearrange("(a p r) k -> a p (r k)", p=P, r=2)
-        m_view = mask.rearrange("(a p r) k -> a p (r k)", p=P, r=2)
-        x_view = x.rearrange("(a p r) k -> a p (r k)", p=P, r=2)
+        w_view = weight.rearrange("(a p r) k -> a p r k", p=P, r=2)
+        m_view = mask.rearrange("(a p r) k -> a p r k", p=P, r=2)
+        x_view = x.rearrange("(a p r) k -> a p r k", p=P, r=2)
         o_view = out.rearrange("(i p) n -> p i n", p=P)
 
-        def transpose_rows(src, dst):
+        def transpose_pass(src, dst, g):
             words = src.bitcast(F32)
             dwords = dst.bitcast(F32)
-            for g in range(G):
-                pt = bank(g, [P, 512])
-                for r in range(2):
-                    for u in range(2):
-                        col = r * 1024 + 256 * g + 128 * u
-                        nc.tensor.transpose(pt[:, (2 * r + u) * P:(2 * r + u + 1) * P], words[:, col:col + P], ident[:])
-                nc.scalar.copy(
-                    out=dwords[:, g * 512:(g + 1) * 512].rearrange("p (j r u) -> p j r u", r=2, u=2),
-                    in_=pt[:].rearrange("p (r u j) -> p j r u", r=2, u=2),
-                )
+            pt = bank(g, [P, 512])
+            for r in range(2):
+                for u in range(2):
+                    col = r * 1024 + 256 * g + 128 * u
+                    nc.tensor.transpose(pt[:, (2 * r + u) * P:(2 * r + u + 1) * P], words[:, col:col + P], ident[:])
+            nc.scalar.copy(
+                out=dwords[:, g * 512:(g + 1) * 512].rearrange("p (j r u) -> p j r u", r=2, u=2),
+                in_=pt[:].rearrange("p (r u j) -> p j r u", r=2, u=2),
+            )
 
         bias_bc = const.tile([P, N], BF16, name="bias_bc")
-        for c in range(4):
-            pb = bank(4 + c, [P, 512])
-            nc.tensor.matmul(pb[:], lhsT=ones_b[:], rhs=brow[:, c * 512:(c + 1) * 512], start=True, stop=True)
-            nc.scalar.copy(out=bias_bc[:, c * 512:(c + 1) * 512], in_=pb[:])
+        n_pieces = [i for i in range(W_LOADS) if KINDS[i] == "N"]
+        for j, i in enumerate(n_pieces):
+            pb = bank(4 + j % 4, [P, ROWS])
+            nc.tensor.matmul(pb[:], lhsT=ones_b[:], rhs=brow[:, i * ROWS:(i + 1) * ROWS], start=True, stop=True)
+            nc.scalar.copy(out=bias_bc[:, i * ROWS:(i + 1) * ROWS], in_=pb[:])
+        bsq = const.tile([P, P], F32, name="bsq")
+        nc.vector.tensor_copy(out=bsq[:], in_=bsq_b[:])
+        pq = bank(0, [P, P])
+        nc.tensor.transpose(pq[:], bsq[:], ident[:])
+        bias_t = const.tile([P, N // P], F32, name="bias_t")
+        nc.scalar.copy(out=bias_t[:], in_=pq[:, 0:N // P])
 
         acc_a = bank(4, [P, ONES_N])
         acc_d = bank(5, [P, P])
         sacc = const.tile([P, 2 * W_LOADS], F32, name="sacc")
+        nc.vector.memset(sacc[:], 0.0)
         aw = []
         sg = []
         n_a = W_LOADS * 32
-        n_d = W_LOADS * 2 * DIAG_BLOCKS
+        n_d = 2 * sum(DIAG_BLOCKS)
+        done_d = [0]
 
         def stage1(a):
             wt = stream.tile([P, 2 * K], BF16, name="wt", tag="w", bufs=4)
             mk = stream.tile([P, 2 * K], BF16, name="mk", tag="m", align_bytes=64)
-            nc.sync.dma_start(out=wt[:], in_=w_view[a])
-            nc.sync.dma_start(out=mk[:], in_=m_view[a])
-            for r in range(2):
-                sl = slice(r * K, (r + 1) * K)
-                nc.vector.tensor_tensor(out=wt[:, sl], in0=wt[:, sl], in1=mk[:, sl], op=ALU.mult)
             aw.append(big.tile([P, PIECE], BF16, name="aw%d" % a, tag="aw", align_bytes=64))
             sg.append(big.tile([P, PIECE], BF16, name="sg%d" % a, tag="sg", align_bytes=64))
-            transpose_rows(wt[:], sg[a][:])
-            for r in range(2):
-                for b in range(DIAG_BLOCKS):
-                    i_d = (a * 2 + r) * DIAG_BLOCKS + b
+            w3 = wt[:].rearrange("p (r k) -> p r k", r=2)
+            m3 = mk[:].rearrange("p (r k) -> p r k", r=2)
+            if a in SPLIT:
+                for hk in range(2):
+                    ks = slice(hk * 1024, (hk + 1) * 1024)
+                    nc.sync.dma_start(out=w3[:, :, ks], in_=w_view[a][:, :, ks])
+                    nc.sync.dma_start(out=m3[:, :, ks], in_=m_view[a][:, :, ks])
+                for g in range(G):
+                    ks = slice(g * 512, (g + 1) * 512)
+                    nc.vector.tensor_tensor(out=w3[:, :, ks], in0=w3[:, :, ks], in1=m3[:, :, ks], op=ALU.mult)
+                    transpose_pass(wt[:], sg[a][:], g)
+            else:
+                nc.sync.dma_start(out=w3, in_=w_view[a])
+                nc.sync.dma_start(out=m3, in_=m_view[a])
+                for r in range(2):
+                    nc.vector.tensor_tensor(out=w3[:, r, :], in0=w3[:, r, :], in1=m3[:, r, :], op=ALU.mult)
+                for g in range(G):
+                    transpose_pass(wt[:], sg[a][:], g)
+            nb = DIAG_BLOCKS[a]
+            for b in range(nb):
+                for r in range(2):
                     blk = wt[:, r * K + b * P:r * K + (b + 1) * P]
-                    nc.tensor.matmul(acc_d[:], lhsT=blk, rhs=blk, start=(i_d == 0), stop=(i_d == n_d - 1))
-                junk = stream.tile([P, SQ_COLS], BF16, name="junk", tag="junk", bufs=2)
-                nc.scalar.activation(
-                    out=junk[:], in_=wt[:, r * K + DIAG_BLOCKS * P:(r + 1) * K], func=ACT.Square,
-                    accum_out=sacc[:, 2 * a + r:2 * a + r + 1],
-                )
+                    nc.tensor.matmul(acc_d[:], lhsT=blk, rhs=blk, start=(done_d[0] == 0), stop=(done_d[0] == n_d - 1))
+                    done_d[0] += 1
+            if nb < 16:
+                for r in range(2):
+                    junk = stream.tile([P, K - nb * P], BF16, name="junk", tag="junk", bufs=2)
+                    nc.scalar.activation(
+                        out=junk[:], in_=wt[:, r * K + nb * P:(r + 1) * K], func=ACT.Square,
+                        accum_out=sacc[:, 2 * a + r:2 * a + r + 1],
+                    )
 
-        def stage2(a):
-            nc.vector.tensor_single_scalar(out=aw[a][:].bitcast(I32), in_=sg[a][:].bitcast(I32), scalar=0x7FFF7FFF, op=ALU.bitwise_and)
+        def magnitude(a):
+            parts = G if a in SPLIT else 1
+            width = PIECE // parts
+            for s in range(parts):
+                sl = slice(s * width, (s + 1) * width)
+                nc.vector.tensor_single_scalar(out=aw[a][:, sl].bitcast(I32), in_=sg[a][:, sl].bitcast(I32), scalar=0x7FFF7FFF, op=ALU.bitwise_and)
+                for q in range(s * 32 // parts, (s + 1) * 32 // parts):
+                    i_a = a * 32 + q
+                    nc.tensor.matmul(acc_a[:], lhsT=aw[a][:, q * P:(q + 1) * P], rhs=ones_b[:, 0:ONES_N], start=(i_a == 0), stop=(i_a == n_a - 1))
+
+        def half_sign(a):
             nc.vector.tensor_scalar(out=sg[a][:], in0=sg[a][:], scalar1=0.0, scalar2=0.5, op0=ALU.is_ge, op1=ALU.subtract)
-            for q in range(32):
-                i_a = a * 32 + q
-                nc.tensor.matmul(acc_a[:], lhsT=aw[a][:, q * P:(q + 1) * P], rhs=ones_b[:, 0:ONES_N], start=(i_a == 0), stop=(i_a == n_a - 1))
 
         for a in range(W_LOADS):
             stage1(a)
             if a >= 1:
-                stage2(a - 1)
-        stage2(W_LOADS - 1)
+                magnitude(a - 1)
+            if a >= 2:
+                half_sign(a - 2)
 
-        zt = const.tile([P, 2 + P], F32, name="zt")
-        nc.vector.tensor_copy(out=zt[:, 0:2], in_=acc_a[:, 0:2])
-        nc.vector.tensor_tensor(out=zt[:, 2:2 + P], in0=acc_d[:], in1=ident[:], op=ALU.mult)
-        tot = bank(6, [P, 2 + P + 2 * W_LOADS])
-        nc.tensor.matmul(tot[:, 2 + P:], lhsT=mean_w[:], rhs=sacc[:], start=True, stop=True)
-        nc.tensor.matmul(tot[:, 0:2 + P], lhsT=mean_w[:], rhs=zt[:], start=True, stop=True)
+        zd = const.tile([P, P], F32, name="zd")
+        nc.vector.tensor_tensor(out=zd[:], in0=acc_d[:], in1=ident[:], op=ALU.mult)
+        tot = bank(6, [P, P + 2 * W_LOADS])
+        nc.tensor.matmul(tot[:, P:], lhsT=mean_w[:], rhs=sacc[:], start=True, stop=True)
+        nc.tensor.matmul(tot[:, 0:P], lhsT=mean_w[:], rhs=zd[:], start=True, stop=True)
         st = const.tile([P, 8], F32, name="st")
-        nc.vector.tensor_reduce(out=st[:, 0:1], in_=tot[:, 2:], axis=mybir.AxisListType.X, op=ALU.add)
-        nc.vector.tensor_copy(out=st[:, 1:2], in_=tot[:, 0:1])
+        nc.vector.tensor_reduce(out=st[:, 0:1], in_=tot[:], axis=mybir.AxisListType.X, op=ALU.add)
+        magnitude(W_LOADS - 1)
+        za = const.tile([P, ONES_N], F32, name="za")
+        nc.vector.tensor_copy(out=za[:], in_=acc_a[:])
+        tm = bank(7, [P, ONES_N])
+        nc.tensor.matmul(tm[:], lhsT=mean_w[:], rhs=za[:], start=True, stop=True)
+        nc.vector.tensor_copy(out=st[:, 1:2], in_=tm[:, 0:1])
         nc.vector.scalar_tensor_tensor(out=st[:, 2:3], in0=st[:, 1:2], scalar=st[:, 1:2], in1=st[:, 0:1], op0=ALU.mult, op1=ALU.subtract)
         nc.vector.tensor_scalar(out=st[:, 3:4], in0=st[:, 2:3], scalar1=-0.25 * COUNT / (COUNT - 1), scalar2=0.0, op0=ALU.mult, op1=ALU.max)
         thr = const.tile([P, 1], F32, name="thr")
         nc.scalar.activation(out=thr[:], in_=st[:, 3:4], func=ACT.Sqrt)
         nc.vector.tensor_scalar(out=st[:, 4:5], in0=st[:, 1:2], scalar1=2.0, scalar2=2e-8, op0=ALU.mult, op1=ALU.add)
+        half_sign(W_LOADS - 2)
+        half_sign(W_LOADS - 1)
 
         xc = const.tile([P, X_LOADS * G * ROWS], U32, name="xc", align_bytes=64)
         xs = const.tile([P, X_LOADS * G * ROWS], U8, name="xs", align_bytes=64)
 
         def load_x(b):
             xt = stream.tile([P, 2 * K], BF16, name="xt", tag="w", bufs=4)
-            nc.sync.dma_start(out=xt[:], in_=x_view[b])
+            nc.sync.dma_start(out=xt[:].rearrange("p (r k) -> p r k", r=2), in_=x_view[b])
             xg = stream.tile([P, PIECE], BF16, name="xg", tag="m", align_bytes=64)
-            transpose_rows(xt[:], xg[:])
+            for g in range(G):
+                transpose_pass(xt[:], xg[:], g)
             sl = slice(b * G * ROWS, (b + 1) * G * ROWS)
             nc.vector.quantize_mx(out=xc[:, sl].bitcast(FP8X4), scales=xs[:, sl], in_=xg[:])
 
         wc = []
         ws = []
-        accs = []
+        accs = {}
+        o_t = {}
 
         def prepare(i):
             if i == 0:
@@ -159,7 +202,7 @@ def tile_masklockedlinear_kernel(tc, x, weight, mask, bias, out):
             nc.vector.tensor_tensor(out=sg[i][:], in0=aw[i][:], in1=sg[i][:], op=ALU.mult)
             nc.vector.quantize_mx(out=wc[i][:].bitcast(FP8X4), scales=ws[i][:], in_=sg[i][:])
 
-        def multiply(i):
+        def multiply_n(i):
             mine = []
             for b in range(X_LOADS):
                 acc = bank(((i + 1) % 2) * 4 + b, [P, 2 * ROWS])
@@ -173,33 +216,81 @@ def tile_masklockedlinear_kernel(tc, x, weight, mask, bias, out):
                             start=(g == 0), stop=(g == G - 1),
                         )
                 mine.append(acc)
-            accs.append(mine)
+            accs[i] = mine
 
-        def finish(i):
+        def store(i, ot, q):
+            nc.sync.dma_start(
+                out=o_view[:, (q - 1) * 2:(q + 1) * 2, i * ROWS:(i + 1) * ROWS],
+                in_=ot[:, (q - 1) * 2 * ROWS:(q + 1) * 2 * ROWS].rearrange("p (i n) -> p i n", i=4),
+            )
+
+        def finish_n(i):
             ot = stream.tile([P, 8 * ROWS], F32, name="ot", tag="w", bufs=4)
-            cols = slice(i * ROWS, (i + 1) * ROWS)
             for b in range(X_LOADS):
                 nc.vector.tensor_tensor(
                     out=ot[:, b * 2 * ROWS:(b + 1) * 2 * ROWS].rearrange("p (h n) -> p h n", h=2),
                     in0=accs[i][b][:].rearrange("p (h n) -> p h n", h=2),
-                    in1=bias_bc[:, cols].unsqueeze(1).to_broadcast([P, 2, ROWS]),
+                    in1=bias_bc[:, i * ROWS:(i + 1) * ROWS].unsqueeze(1).to_broadcast([P, 2, ROWS]),
                     op=ALU.add,
                 )
                 if b % 2 == 1:
-                    nc.sync.dma_start(
-                        out=o_view[:, (b - 1) * 2:(b + 1) * 2, cols],
-                        in_=ot[:, (b - 1) * 2 * ROWS:(b + 1) * 2 * ROWS].rearrange("p (i n) -> p i n", i=4),
+                    store(i, ot, b)
+
+        def multiply_t(i):
+            base = ((i + 1) % 2) * 4
+            o_t[i] = stream.tile([P, 2 * M], F32, name="o_t", tag="m", align_bytes=64)
+            for mh in range(2):
+                for nt in range(2):
+                    acc = bank(base + mh * 2 + nt, [P, 2 * ROWS])
+                    for bb in range(2):
+                        for g in range(G):
+                            lo = g * ROWS + nt * P
+                            xo = (mh * 2 + bb) * G * ROWS + g * ROWS
+                            nc.tensor.matmul_mx(
+                                out=acc[:, bb * ROWS:(bb + 1) * ROWS],
+                                lhsT=wc[i][:, lo:lo + P].bitcast(FP8X4), lhsT_scale=ws[i][:, lo:lo + P],
+                                rhs=xc[:, xo:xo + ROWS].bitcast(FP8X4), rhs_scale=xs[:, xo:xo + ROWS],
+                                start=(g == 0), stop=(g == G - 1),
+                            )
+                    nc.scalar.activation(
+                        out=o_t[i][:, nt * M + mh * 512:nt * M + (mh + 1) * 512], in_=acc[:], func=ACT.Identity,
+                        bias=bias_t[:, 2 * i + nt:2 * i + nt + 1], scale=1.0,
                     )
+
+        def finish_t(i):
+            base = ((i + 1) % 2) * 4
+            ot = stream.tile([P, 8 * ROWS], F32, name="ot", tag="w", bufs=4)
+            for q in range(4):
+                bt = bank(base + q, [P, 2 * ROWS])
+                for h in range(2):
+                    for nt in range(2):
+                        mo = nt * M + (2 * q + h) * P
+                        nc.tensor.transpose(bt[:, h * ROWS + nt * P:h * ROWS + (nt + 1) * P], o_t[i][:, mo:mo + P], ident[:])
+                nc.scalar.copy(out=ot[:, q * 2 * ROWS:(q + 1) * 2 * ROWS], in_=bt[:])
+                if q % 2 == 1:
+                    store(i, ot, q)
+
+        def mult(i):
+            if KINDS[i] == "T":
+                multiply_t(i)
+            else:
+                multiply_n(i)
+
+        def fin(i):
+            if KINDS[i] == "T":
+                finish_t(i)
+            else:
+                finish_n(i)
 
         prepare(0)
         for b in range(X_LOADS):
             load_x(b)
-        multiply(0)
+        mult(0)
         prepare(1)
-        multiply(1)
+        mult(1)
         for i in range(2, W_LOADS):
-            finish(i - 2)
+            fin(i - 2)
             prepare(i)
-            multiply(i)
-        finish(W_LOADS - 2)
-        finish(W_LOADS - 1)
+            mult(i)
+        fin(W_LOADS - 2)
+        fin(W_LOADS - 1)

@@ -22,11 +22,10 @@ W_LOADS = N // ROWS
 X_LOADS = M // ROWS
 PIECE = G * ROWS * 4
 COUNT = N * K
-DIAG_BLOCKS = [10, 10, 10, 10, 10, 10, 10, 16]
+DIAG_BLOCKS = 10
 ONES_N = 2
-KINDS = "TNTTNTTN"
-SPLIT = [0, W_LOADS - 1]
-LATE_SIGN = 3
+KINDS = "NTNTNTNN"
+LAST = W_LOADS - 1
 
 
 def tile_masklockedlinear_kernel(tc, x, weight, mask, bias, out):
@@ -36,16 +35,44 @@ def tile_masklockedlinear_kernel(tc, x, weight, mask, bias, out):
         stream = ctx.enter_context(tc.tile_pool(name="stream", bufs=3))
         big = ctx.enter_context(tc.tile_pool(name="big", bufs=W_LOADS))
         psum = ctx.enter_context(tc.psum_pool(name="psum", bufs=1))
+        ctx.enter_context(tc.manual_schedule())
 
         def bank(i, shape):
             return psum.tile(shape, F32, name="bank%d" % i, tag="bank%d" % i)
 
+        w_view = weight.rearrange("(a p r) k -> a p r k", p=P, r=2)
+        m_view = mask.rearrange("(a p r) k -> a p r k", p=P, r=2)
+        x_view = x.rearrange("(a p r) k -> a p r k", p=P, r=2)
+        o_view = out.rearrange("(i p) n -> p i n", p=P)
+
+        wt = {}
+        mk = {}
+        aw = {}
+        sg = {}
+
+        def load_w(a):
+            wt[a] = stream.tile([P, 2 * K], BF16, name="wt", tag="w", bufs=4)
+            mk[a] = stream.tile([P, 2 * K], BF16, name="mk", tag="m", align_bytes=64)
+            w3 = wt[a][:].rearrange("p (r k) -> p r k", r=2)
+            m3 = mk[a][:].rearrange("p (r k) -> p r k", r=2)
+            if a in (0, LAST):
+                for hk in range(2):
+                    ks = slice(hk * 1024, (hk + 1) * 1024)
+                    nc.sync.dma_start(out=w3[:, :, ks], in_=w_view[a][:, :, ks])
+                    nc.sync.dma_start(out=m3[:, :, ks], in_=m_view[a][:, :, ks])
+            else:
+                nc.sync.dma_start(out=w3, in_=w_view[a])
+                nc.sync.dma_start(out=m3, in_=m_view[a])
+
         brow = const.tile([P, N], BF16, name="brow")
         nc.vector.memset(brow[:], 0.0)
-        nc.sync.dma_start(out=brow[0:1, :], in_=bias.rearrange("(o n) -> o n", o=1))
+        nc.scalar.dma_start(out=brow[0:1, :], in_=bias.rearrange("(o n) -> o n", o=1))
         bsq_b = const.tile([P, P], BF16, name="bsq_b")
         nc.vector.memset(bsq_b[:], 0.0)
-        nc.sync.dma_start(out=bsq_b[0:N // P, :], in_=bias.rearrange("(t n) -> t n", n=P))
+        nc.scalar.dma_start(out=bsq_b[0:N // P, :], in_=bias.rearrange("(t n) -> t n", n=P))
+        load_w(0)
+        load_w(1)
+        load_w(2)
         ident = const.tile([P, P], F32, name="ident")
         make_identity(nc, ident[:])
         mean_w = const.tile([P, P], F32, name="mean_w")
@@ -54,11 +81,7 @@ def tile_masklockedlinear_kernel(tc, x, weight, mask, bias, out):
         nc.vector.memset(ones_b[:], 1.0)
         warm = const.tile([P, 1], F32, name="warm")
         nc.scalar.activation(out=warm[:], in_=mean_w[:, 0:1], func=ACT.Sqrt)
-
-        w_view = weight.rearrange("(a p r) k -> a p r k", p=P, r=2)
-        m_view = mask.rearrange("(a p r) k -> a p r k", p=P, r=2)
-        x_view = x.rearrange("(a p r) k -> a p r k", p=P, r=2)
-        o_view = out.rearrange("(i p) n -> p i n", p=P)
+        sacc = const.tile([P, 2 * W_LOADS], F32, name="sacc")
 
         def transpose_pass(src, dst, g):
             words = src.bitcast(F32)
@@ -88,160 +111,206 @@ def tile_masklockedlinear_kernel(tc, x, weight, mask, bias, out):
 
         acc_a = bank(4, [P, ONES_N])
         acc_d = bank(5, [P, P])
-        sacc = const.tile([P, 2 * W_LOADS], F32, name="sacc")
-        nc.vector.memset(sacc[:], 0.0)
-        aw = []
-        sg = []
         n_a = W_LOADS * 32
-        n_d = 2 * sum(DIAG_BLOCKS)
-        done_d = [0]
+        n_d = W_LOADS * 2 * DIAG_BLOCKS
 
-        def stage1(a):
-            wt = stream.tile([P, 2 * K], BF16, name="wt", tag="w", bufs=4)
-            mk = stream.tile([P, 2 * K], BF16, name="mk", tag="m", align_bytes=64)
-            aw.append(big.tile([P, PIECE], BF16, name="aw%d" % a, tag="aw", align_bytes=64))
-            sg.append(big.tile([P, PIECE], BF16, name="sg%d" % a, tag="sg", align_bytes=64))
-            w3 = wt[:].rearrange("p (r k) -> p r k", r=2)
-            m3 = mk[:].rearrange("p (r k) -> p r k", r=2)
-            if a in SPLIT:
-                for hk in range(2):
-                    ks = slice(hk * 1024, (hk + 1) * 1024)
-                    nc.sync.dma_start(out=w3[:, :, ks], in_=w_view[a][:, :, ks])
-                    nc.sync.dma_start(out=m3[:, :, ks], in_=m_view[a][:, :, ks])
-                for g in range(G):
-                    ks = slice(g * 512, (g + 1) * 512)
-                    nc.vector.tensor_tensor(out=w3[:, :, ks], in0=w3[:, :, ks], in1=m3[:, :, ks], op=ALU.mult)
-                    transpose_pass(wt[:], sg[a][:], g)
-            else:
-                nc.sync.dma_start(out=w3, in_=w_view[a])
-                nc.sync.dma_start(out=m3, in_=m_view[a])
-                for r in range(2):
-                    nc.vector.tensor_tensor(out=w3[:, r, :], in0=w3[:, r, :], in1=m3[:, r, :], op=ALU.mult)
-                for g in range(G):
-                    transpose_pass(wt[:], sg[a][:], g)
-            nb = DIAG_BLOCKS[a]
-            for b in range(nb):
-                for r in range(2):
-                    blk = wt[:, r * K + b * P:r * K + (b + 1) * P]
-                    nc.tensor.matmul(acc_d[:], lhsT=blk, rhs=blk, start=(done_d[0] == 0), stop=(done_d[0] == n_d - 1))
-                    done_d[0] += 1
-            if nb < 16:
-                for r in range(2):
-                    junk = stream.tile([P, K - nb * P], BF16, name="junk", tag="junk", bufs=2)
-                    nc.scalar.activation(
-                        out=junk[:], in_=wt[:, r * K + nb * P:(r + 1) * K], func=ACT.Square,
-                        accum_out=sacc[:, 2 * a + r:2 * a + r + 1],
-                    )
+        def new_piece(a):
+            aw[a] = big.tile([P, PIECE], BF16, name="aw%d" % a, tag="aw", align_bytes=64)
+            sg[a] = big.tile([P, PIECE], BF16, name="sg%d" % a, tag="sg", align_bytes=64)
 
-        def magnitude(a):
-            parts = G if a in SPLIT else 1
-            width = PIECE // parts
-            for s in range(parts):
-                sl = slice(s * width, (s + 1) * width)
-                nc.vector.tensor_single_scalar(out=aw[a][:, sl].bitcast(I32), in_=sg[a][:, sl].bitcast(I32), scalar=0x7FFF7FFF, op=ALU.bitwise_and)
-                for q in range(s * 32 // parts, (s + 1) * 32 // parts):
-                    i_a = a * 32 + q
-                    nc.tensor.matmul(acc_a[:], lhsT=aw[a][:, q * P:(q + 1) * P], rhs=ones_b[:, 0:ONES_N], start=(i_a == 0), stop=(i_a == n_a - 1))
+        def mask_rows(a):
+            for r in range(2):
+                sl = slice(r * K, (r + 1) * K)
+                nc.vector.tensor_tensor(out=wt[a][:, sl], in0=wt[a][:, sl], in1=mk[a][:, sl], op=ALU.mult)
+
+        def mask_pass(a, g):
+            w3 = wt[a][:].rearrange("p (r k) -> p r k", r=2)[:, :, g * 512:(g + 1) * 512]
+            m3 = mk[a][:].rearrange("p (r k) -> p r k", r=2)[:, :, g * 512:(g + 1) * 512]
+            nc.vector.tensor_tensor(out=w3, in0=w3, in1=m3, op=ALU.mult)
+
+        def squares_pe(a):
+            for b in range(DIAG_BLOCKS):
+                for r in range(2):
+                    i_d = (a * DIAG_BLOCKS + b) * 2 + r
+                    blk = wt[a][:, r * K + b * P:r * K + (b + 1) * P]
+                    nc.tensor.matmul(acc_d[:], lhsT=blk, rhs=blk, start=(i_d == 0), stop=(i_d == n_d - 1))
+
+        def squares_act(a):
+            for r in range(2):
+                junk = stream.tile([P, K - DIAG_BLOCKS * P], BF16, name="junk", tag="junk", bufs=2)
+                nc.scalar.activation(
+                    out=junk[:], in_=wt[a][:, r * K + DIAG_BLOCKS * P:(r + 1) * K], func=ACT.Square,
+                    accum_out=sacc[:, 2 * a + r:2 * a + r + 1],
+                )
+
+        def magnitude(a, lo, hi):
+            sl = slice(lo * 1024, hi * 1024)
+            nc.vector.tensor_single_scalar(out=aw[a][:, sl].bitcast(I32), in_=sg[a][:, sl].bitcast(I32), scalar=0x7FFF7FFF, op=ALU.bitwise_and)
+
+        def sum_magnitude(a, lo, hi):
+            for q in range(lo * 8, hi * 8):
+                i_a = a * 32 + q
+                nc.tensor.matmul(acc_a[:], lhsT=aw[a][:, q * P:(q + 1) * P], rhs=ones_b[:, 0:ONES_N], start=(i_a == 0), stop=(i_a == n_a - 1))
 
         def half_sign(a):
             nc.vector.tensor_scalar(out=sg[a][:], in0=sg[a][:], scalar1=0.0, scalar2=0.5, op0=ALU.is_ge, op1=ALU.subtract)
 
-        for a in range(W_LOADS):
-            stage1(a)
-            if a >= 1:
-                magnitude(a - 1)
-            if a >= 2:
-                half_sign(a - 2)
-
-        zd = const.tile([P, P], F32, name="zd")
-        nc.vector.tensor_tensor(out=zd[:], in0=acc_d[:], in1=ident[:], op=ALU.mult)
-        tot = bank(6, [P, P + 2 * W_LOADS])
-        nc.tensor.matmul(tot[:, P:], lhsT=mean_w[:], rhs=sacc[:], start=True, stop=True)
-        nc.tensor.matmul(tot[:, 0:P], lhsT=mean_w[:], rhs=zd[:], start=True, stop=True)
-        st = const.tile([P, 8], F32, name="st")
-        nc.vector.tensor_reduce(out=st[:, 0:1], in_=tot[:], axis=mybir.AxisListType.X, op=ALU.add)
-        magnitude(W_LOADS - 1)
-        za = const.tile([P, ONES_N], F32, name="za")
-        nc.vector.tensor_copy(out=za[:], in_=acc_a[:])
-        tm = bank(7, [P, ONES_N])
-        nc.tensor.matmul(tm[:], lhsT=mean_w[:], rhs=za[:], start=True, stop=True)
-        nc.vector.tensor_copy(out=st[:, 1:2], in_=tm[:, 0:1])
-        nc.vector.scalar_tensor_tensor(out=st[:, 2:3], in0=st[:, 1:2], scalar=st[:, 1:2], in1=st[:, 0:1], op0=ALU.mult, op1=ALU.subtract)
-        nc.vector.tensor_scalar(out=st[:, 3:4], in0=st[:, 2:3], scalar1=-0.25 * COUNT / (COUNT - 1), scalar2=0.0, op0=ALU.mult, op1=ALU.max)
-        thr = const.tile([P, 1], F32, name="thr")
-        nc.scalar.activation(out=thr[:], in_=st[:, 3:4], func=ACT.Sqrt)
-        nc.vector.tensor_scalar(out=st[:, 4:5], in0=st[:, 1:2], scalar1=2.0, scalar2=2e-8, op0=ALU.mult, op1=ALU.add)
-        half_sign(W_LOADS - 2)
-        half_sign(W_LOADS - 1)
+        new_piece(0)
+        for g in range(G):
+            mask_pass(0, g)
+            transpose_pass(wt[0][:], sg[0][:], g)
+        squares_pe(0)
+        squares_act(0)
+        for g in range(G):
+            magnitude(0, g, g + 1)
+            sum_magnitude(0, g, g + 1)
+        half_sign(0)
+        load_w(3)
+        new_piece(1)
+        mask_rows(1)
+        for g in range(G):
+            transpose_pass(wt[1][:], sg[1][:], g)
+        squares_pe(1)
+        squares_act(1)
+        for a in range(2, LAST):
+            if a + 2 <= LAST:
+                load_w(a + 2)
+            new_piece(a)
+            mask_rows(a)
+            for g in range(G):
+                transpose_pass(wt[a][:], sg[a][:], g)
+            magnitude(a - 1, 0, G)
+            squares_pe(a)
+            squares_act(a)
+            sum_magnitude(a - 1, 0, G)
+            if a < LAST - 1:
+                half_sign(a - 1)
 
         xc = const.tile([P, X_LOADS * G * ROWS], U32, name="xc", align_bytes=64)
         xs = const.tile([P, X_LOADS * G * ROWS], U8, name="xs", align_bytes=64)
+        xt = {}
+        xg = {}
 
         def load_x(b):
-            xt = stream.tile([P, 2 * K], BF16, name="xt", tag="w", bufs=4)
-            nc.sync.dma_start(out=xt[:].rearrange("p (r k) -> p r k", r=2), in_=x_view[b])
-            xg = stream.tile([P, PIECE], BF16, name="xg", tag="m", align_bytes=64)
-            for g in range(G):
-                transpose_pass(xt[:], xg[:], g)
-            sl = slice(b * G * ROWS, (b + 1) * G * ROWS)
-            nc.vector.quantize_mx(out=xc[:, sl].bitcast(FP8X4), scales=xs[:, sl], in_=xg[:])
+            xt[b] = stream.tile([P, 2 * K], BF16, name="xt", tag="w", bufs=4)
+            nc.sync.dma_start(out=xt[b][:].rearrange("p (r k) -> p r k", r=2), in_=x_view[b])
 
-        wc = []
-        ws = []
+        def transpose_x(b, g):
+            if g == 0:
+                xg[b] = stream.tile([P, PIECE], BF16, name="xg", tag="m", align_bytes=64)
+            transpose_pass(xt[b][:], xg[b][:], g)
+
+        def quantise_x(b):
+            sl = slice(b * G * ROWS, (b + 1) * G * ROWS)
+            nc.vector.quantize_mx(out=xc[:, sl].bitcast(FP8X4), scales=xs[:, sl], in_=xg[b][:])
+
+        for b in range(3):
+            load_x(b)
+        new_piece(LAST)
+        for g in range(G):
+            mask_pass(LAST, g)
+            transpose_pass(wt[LAST][:], sg[LAST][:], g)
+        half_sign(LAST - 2)
+        magnitude(LAST - 1, 0, G)
+        squares_pe(LAST)
+        squares_act(LAST)
+        load_x(3)
+        sum_magnitude(LAST - 1, 0, G)
+        for g in range(G):
+            magnitude(LAST, g, g + 1)
+            sum_magnitude(LAST, g, g + 1)
+            if g == 1:
+                half_sign(LAST - 1)
+        half_sign(LAST)
+
+        zd = const.tile([P, P], F32, name="zd")
+        nc.vector.tensor_tensor(out=zd[:], in0=acc_d[:], in1=ident[:], op=ALU.mult)
+        za = const.tile([P, ONES_N], F32, name="za")
+        nc.vector.tensor_copy(out=za[:], in_=acc_a[:])
+        tot = bank(6, [P, P + 2 * W_LOADS])
+        nc.tensor.matmul(tot[:, P:], lhsT=mean_w[:], rhs=sacc[:], start=True, stop=True)
+        transpose_x(0, 0)
+        transpose_x(0, 1)
+        nc.tensor.matmul(tot[:, 0:P], lhsT=mean_w[:], rhs=zd[:], start=True, stop=True)
+        tm = bank(7, [P, ONES_N])
+        nc.tensor.matmul(tm[:], lhsT=mean_w[:], rhs=za[:], start=True, stop=True)
+        transpose_x(0, 2)
+        transpose_x(0, 3)
+        st = const.tile([P, 8], F32, name="st")
+        nc.vector.tensor_reduce(out=st[:, 0:1], in_=tot[:], axis=mybir.AxisListType.X, op=ALU.add)
+        nc.vector.tensor_copy(out=st[:, 1:2], in_=tm[:, 0:1])
+        nc.vector.scalar_tensor_tensor(out=st[:, 2:3], in0=st[:, 1:2], scalar=st[:, 1:2], in1=st[:, 0:1], op0=ALU.mult, op1=ALU.subtract)
+        nc.vector.tensor_scalar(out=st[:, 4:5], in0=st[:, 1:2], scalar1=2.0, scalar2=2e-8, op0=ALU.mult, op1=ALU.add)
+        nc.vector.tensor_scalar(out=st[:, 3:4], in0=st[:, 2:3], scalar1=-0.25 * COUNT / (COUNT - 1), scalar2=0.0, op0=ALU.mult, op1=ALU.max)
+        thr = const.tile([P, 1], F32, name="thr")
+        nc.scalar.activation(out=thr[:], in_=st[:, 3:4], func=ACT.Sqrt)
+        for b in (1, 2):
+            for g in range(G):
+                transpose_x(b, g)
+        quantise_x(0)
+        for g in range(G):
+            transpose_x(3, g)
+
+        wc = {}
+        ws = {}
         accs = {}
         o_t = {}
+        ots = {}
 
-        def prepare(i):
-            if i == 0:
-                wc.append(const.tile([P, G * ROWS], U32, name="wc0", align_bytes=64))
-                ws.append(const.tile([P, G * ROWS], U8, name="ws0", align_bytes=64))
-            else:
-                wc.append(big.tile([P, G * ROWS], U32, name="wc%d" % i, tag="aw", align_bytes=64))
-                ws.append(big.tile([P, G * ROWS], U8, name="ws%d" % i, tag="sg", align_bytes=64))
+        def threshold(i):
             nc.vector.tensor_scalar(out=aw[i][:], in0=aw[i][:], scalar1=thr[:, 0:1], scalar2=st[:, 4:5], op0=ALU.is_gt, op1=ALU.mult)
+
+        def signed(i):
             nc.vector.tensor_tensor(out=sg[i][:], in0=aw[i][:], in1=sg[i][:], op=ALU.mult)
+
+        def quantise_w(i):
+            if i == 0:
+                wc[i] = const.tile([P, G * ROWS], U32, name="wc0", align_bytes=64)
+                ws[i] = const.tile([P, G * ROWS], U8, name="ws0", align_bytes=64)
+            else:
+                wc[i] = big.tile([P, G * ROWS], U32, name="wc%d" % i, tag="aw", align_bytes=64)
+                ws[i] = big.tile([P, G * ROWS], U8, name="ws%d" % i, tag="sg", align_bytes=64)
             nc.vector.quantize_mx(out=wc[i][:].bitcast(FP8X4), scales=ws[i][:], in_=sg[i][:])
 
-        def multiply_n(i):
-            mine = []
-            for b in range(X_LOADS):
-                acc = bank(((i + 1) % 2) * 4 + b, [P, 2 * ROWS])
-                for h in range(2):
-                    for g in range(G):
-                        lo = b * G * ROWS + g * ROWS + h * P
-                        nc.tensor.matmul_mx(
-                            out=acc[:, h * ROWS:(h + 1) * ROWS],
-                            lhsT=xc[:, lo:lo + P].bitcast(FP8X4), lhsT_scale=xs[:, lo:lo + P],
-                            rhs=wc[i][:, g * ROWS:(g + 1) * ROWS].bitcast(FP8X4), rhs_scale=ws[i][:, g * ROWS:(g + 1) * ROWS],
-                            start=(g == 0), stop=(g == G - 1),
-                        )
-                mine.append(acc)
-            accs[i] = mine
+        def base(i):
+            return ((i + 1) % 2) * 4
 
-        def store(i, ot, q):
+        def multiply_n(i, b):
+            acc = bank(base(i) + b, [P, 2 * ROWS])
+            for h in range(2):
+                for g in range(G):
+                    lo = b * G * ROWS + g * ROWS + h * P
+                    nc.tensor.matmul_mx(
+                        out=acc[:, h * ROWS:(h + 1) * ROWS],
+                        lhsT=xc[:, lo:lo + P].bitcast(FP8X4), lhsT_scale=xs[:, lo:lo + P],
+                        rhs=wc[i][:, g * ROWS:(g + 1) * ROWS].bitcast(FP8X4), rhs_scale=ws[i][:, g * ROWS:(g + 1) * ROWS],
+                        start=(g == 0), stop=(g == G - 1),
+                    )
+            accs[(i, b)] = acc
+
+        def store(i, q):
             nc.sync.dma_start(
                 out=o_view[:, (q - 1) * 2:(q + 1) * 2, i * ROWS:(i + 1) * ROWS],
-                in_=ot[:, (q - 1) * 2 * ROWS:(q + 1) * 2 * ROWS].rearrange("p (i n) -> p i n", i=4),
+                in_=ots[i][:, (q - 1) * 2 * ROWS:(q + 1) * 2 * ROWS].rearrange("p (i n) -> p i n", i=4),
             )
 
-        def finish_n(i):
-            ot = stream.tile([P, 8 * ROWS], F32, name="ot", tag="w", bufs=4)
-            for b in range(X_LOADS):
-                nc.vector.tensor_tensor(
-                    out=ot[:, b * 2 * ROWS:(b + 1) * 2 * ROWS].rearrange("p (h n) -> p h n", h=2),
-                    in0=accs[i][b][:].rearrange("p (h n) -> p h n", h=2),
-                    in1=bias_bc[:, i * ROWS:(i + 1) * ROWS].unsqueeze(1).to_broadcast([P, 2, ROWS]),
-                    op=ALU.add,
-                )
-                if b % 2 == 1:
-                    store(i, ot, b)
+        def finish_n(i, b):
+            if b == 0:
+                ots[i] = stream.tile([P, 8 * ROWS], F32, name="ot", tag="w", bufs=4)
+            nc.vector.tensor_tensor(
+                out=ots[i][:, b * 2 * ROWS:(b + 1) * 2 * ROWS].rearrange("p (h n) -> p h n", h=2),
+                in0=accs[(i, b)][:].rearrange("p (h n) -> p h n", h=2),
+                in1=bias_bc[:, i * ROWS:(i + 1) * ROWS].unsqueeze(1).to_broadcast([P, 2, ROWS]),
+                op=ALU.add,
+            )
+            if b % 2 == 1:
+                store(i, b)
 
         def multiply_t(i):
-            base = ((i + 1) % 2) * 4
             o_t[i] = stream.tile([P, 2 * M], F32, name="o_t", tag="m", align_bytes=64)
             for mh in range(2):
                 for nt in range(2):
-                    acc = bank(base + mh * 2 + nt, [P, 2 * ROWS])
+                    acc = bank(base(i) + mh * 2 + nt, [P, 2 * ROWS])
                     for bb in range(2):
                         for g in range(G):
                             lo = g * ROWS + nt * P
@@ -258,39 +327,63 @@ def tile_masklockedlinear_kernel(tc, x, weight, mask, bias, out):
                     )
 
         def finish_t(i):
-            base = ((i + 1) % 2) * 4
-            ot = stream.tile([P, 8 * ROWS], F32, name="ot", tag="w", bufs=4)
+            ots[i] = stream.tile([P, 8 * ROWS], F32, name="ot", tag="w", bufs=4)
             for q in range(4):
-                bt = bank(base + q, [P, 2 * ROWS])
+                bt = bank(base(i) + q, [P, 2 * ROWS])
                 for h in range(2):
                     for nt in range(2):
                         mo = nt * M + (2 * q + h) * P
                         nc.tensor.transpose(bt[:, h * ROWS + nt * P:h * ROWS + (nt + 1) * P], o_t[i][:, mo:mo + P], ident[:])
-                nc.scalar.copy(out=ot[:, q * 2 * ROWS:(q + 1) * 2 * ROWS], in_=bt[:])
+                nc.scalar.copy(out=ots[i][:, q * 2 * ROWS:(q + 1) * 2 * ROWS], in_=bt[:])
                 if q % 2 == 1:
-                    store(i, ot, q)
+                    store(i, q)
 
-        def mult(i):
+        pending = []
+        drained = [0]
+
+        def multiply(i):
             if KINDS[i] == "T":
                 multiply_t(i)
             else:
-                multiply_n(i)
+                for b in range(X_LOADS):
+                    multiply_n(i, b)
+                    pending.append((i, b))
 
-        def fin(i):
-            if KINDS[i] == "T":
-                finish_t(i)
-            else:
-                finish_n(i)
+        def drain(count):
+            for j in range(min(count, len(pending) - drained[0])):
+                i, b = pending[drained[0]]
+                drained[0] += 1
+                finish_n(i, b)
 
-        prepare(0)
+        threshold(0)
+        threshold(1)
+        signed(0)
+        quantise_x(1)
+        quantise_w(0)
+        signed(1)
+        multiply_n(0, 0)
+        multiply_n(0, 1)
+        quantise_x(2)
+        quantise_w(1)
+        quantise_x(3)
+        multiply_n(0, 2)
+        multiply_n(0, 3)
         for b in range(X_LOADS):
-            load_x(b)
-        mult(0)
-        prepare(1)
-        mult(1)
-        for i in range(2, W_LOADS):
-            fin(i - 2)
-            prepare(i)
-            mult(i)
-        fin(W_LOADS - 2)
-        fin(W_LOADS - 1)
+            pending.append((0, b))
+        multiply(1)
+        for i in range(2, W_LOADS, 2):
+            threshold(i)
+            drain(1)
+            signed(i)
+            threshold(i + 1)
+            quantise_w(i)
+            drain(1)
+            signed(i + 1)
+            drain(1)
+            quantise_w(i + 1)
+            drain(1)
+            if KINDS[i - 1] == "T":
+                finish_t(i - 1)
+            multiply(i)
+            multiply(i + 1)
+        drain(len(pending))

@@ -23,9 +23,9 @@ X_LOADS = M // ROWS
 PIECE = G * ROWS * 4
 COUNT = N * K
 DIAG_BLOCKS = 10
-ONES_N = 2
-KINDS = "NTNTNTNN"
-LAST = W_LOADS - 1
+SQ_COLS = K - DIAG_BLOCKS * P
+ONES_N = 8
+KINDS = "TNTTNTTN"
 
 
 def tile_masklockedlinear_kernel(tc, x, weight, mask, bias, out):
@@ -35,44 +35,13 @@ def tile_masklockedlinear_kernel(tc, x, weight, mask, bias, out):
         stream = ctx.enter_context(tc.tile_pool(name="stream", bufs=3))
         big = ctx.enter_context(tc.tile_pool(name="big", bufs=W_LOADS))
         psum = ctx.enter_context(tc.psum_pool(name="psum", bufs=1))
-        ctx.enter_context(tc.manual_schedule())
 
         def bank(i, shape):
             return psum.tile(shape, F32, name="bank%d" % i, tag="bank%d" % i)
 
-        w_view = weight.rearrange("(a p r) k -> a p r k", p=P, r=2)
-        m_view = mask.rearrange("(a p r) k -> a p r k", p=P, r=2)
-        x_view = x.rearrange("(a p r) k -> a p r k", p=P, r=2)
-        o_view = out.rearrange("(i p) n -> p i n", p=P)
-
-        wt = {}
-        mk = {}
-        aw = {}
-        sg = {}
-
-        def load_w(a):
-            wt[a] = stream.tile([P, 2 * K], BF16, name="wt", tag="w", bufs=4)
-            mk[a] = stream.tile([P, 2 * K], BF16, name="mk", tag="m", align_bytes=64)
-            w3 = wt[a][:].rearrange("p (r k) -> p r k", r=2)
-            m3 = mk[a][:].rearrange("p (r k) -> p r k", r=2)
-            if a in (0, LAST):
-                for hk in range(2):
-                    ks = slice(hk * 1024, (hk + 1) * 1024)
-                    nc.sync.dma_start(out=w3[:, :, ks], in_=w_view[a][:, :, ks])
-                    nc.sync.dma_start(out=m3[:, :, ks], in_=m_view[a][:, :, ks])
-            else:
-                nc.sync.dma_start(out=w3, in_=w_view[a])
-                nc.sync.dma_start(out=m3, in_=m_view[a])
-
         brow = const.tile([P, N], BF16, name="brow")
         nc.vector.memset(brow[:], 0.0)
-        nc.scalar.dma_start(out=brow[0:1, :], in_=bias.rearrange("(o n) -> o n", o=1))
-        bsq_b = const.tile([P, P], BF16, name="bsq_b")
-        nc.vector.memset(bsq_b[:], 0.0)
-        nc.scalar.dma_start(out=bsq_b[0:N // P, :], in_=bias.rearrange("(t n) -> t n", n=P))
-        load_w(0)
-        load_w(1)
-        load_w(2)
+        nc.sync.dma_start(out=brow[0:1, :], in_=bias.rearrange("(o n) -> o n", o=1))
         ident = const.tile([P, P], F32, name="ident")
         make_identity(nc, ident[:])
         mean_w = const.tile([P, P], F32, name="mean_w")
@@ -81,27 +50,35 @@ def tile_masklockedlinear_kernel(tc, x, weight, mask, bias, out):
         nc.vector.memset(ones_b[:], 1.0)
         warm = const.tile([P, 1], F32, name="warm")
         nc.scalar.activation(out=warm[:], in_=mean_w[:, 0:1], func=ACT.Sqrt)
-        sacc = const.tile([P, 2 * W_LOADS], F32, name="sacc")
 
-        def transpose_pass(src, dst, g):
+        w_view = weight.rearrange("(a p r) k -> a p (r k)", p=P, r=2)
+        m_view = mask.rearrange("(a p r) k -> a p (r k)", p=P, r=2)
+        x_view = x.rearrange("(a p r) k -> a p (r k)", p=P, r=2)
+        o_view = out.rearrange("(i p) n -> p i n", p=P)
+
+        def transpose_rows(src, dst):
             words = src.bitcast(F32)
             dwords = dst.bitcast(F32)
-            pt = bank(g, [P, 512])
-            for r in range(2):
-                for u in range(2):
-                    col = r * 1024 + 256 * g + 128 * u
-                    nc.tensor.transpose(pt[:, (2 * r + u) * P:(2 * r + u + 1) * P], words[:, col:col + P], ident[:])
-            nc.scalar.copy(
-                out=dwords[:, g * 512:(g + 1) * 512].rearrange("p (j r u) -> p j r u", r=2, u=2),
-                in_=pt[:].rearrange("p (r u j) -> p j r u", r=2, u=2),
-            )
+            for g in range(G):
+                pt = bank(g, [P, 512])
+                for r in range(2):
+                    for u in range(2):
+                        col = r * 1024 + 256 * g + 128 * u
+                        nc.tensor.transpose(pt[:, (2 * r + u) * P:(2 * r + u + 1) * P], words[:, col:col + P], ident[:])
+                nc.scalar.copy(
+                    out=dwords[:, g * 512:(g + 1) * 512].rearrange("p (j r u) -> p j r u", r=2, u=2),
+                    in_=pt[:].rearrange("p (r u j) -> p j r u", r=2, u=2),
+                )
 
         bias_bc = const.tile([P, N], BF16, name="bias_bc")
-        n_pieces = [i for i in range(W_LOADS) if KINDS[i] == "N"]
-        for j, i in enumerate(n_pieces):
-            pb = bank(4 + j % 4, [P, ROWS])
-            nc.tensor.matmul(pb[:], lhsT=ones_b[:], rhs=brow[:, i * ROWS:(i + 1) * ROWS], start=True, stop=True)
-            nc.scalar.copy(out=bias_bc[:, i * ROWS:(i + 1) * ROWS], in_=pb[:])
+        for c in range(4):
+            pb = bank(4 + c, [P, 512])
+            nc.tensor.matmul(pb[:], lhsT=ones_b[:], rhs=brow[:, c * 512:(c + 1) * 512], start=True, stop=True)
+            nc.scalar.copy(out=bias_bc[:, c * 512:(c + 1) * 512], in_=pb[:])
+
+        bsq_b = const.tile([P, P], BF16, name="bsq_b")
+        nc.vector.memset(bsq_b[:], 0.0)
+        nc.sync.dma_start(out=bsq_b[0:N // P, :], in_=bias.rearrange("(t n) -> t n", n=P))
         bsq = const.tile([P, P], F32, name="bsq")
         nc.vector.tensor_copy(out=bsq[:], in_=bsq_b[:])
         pq = bank(0, [P, P])
@@ -111,206 +88,128 @@ def tile_masklockedlinear_kernel(tc, x, weight, mask, bias, out):
 
         acc_a = bank(4, [P, ONES_N])
         acc_d = bank(5, [P, P])
+        sacc = const.tile([P, 2 * W_LOADS], F32, name="sacc")
+        aw = []
+        sg = []
         n_a = W_LOADS * 32
         n_d = W_LOADS * 2 * DIAG_BLOCKS
 
-        def new_piece(a):
-            aw[a] = big.tile([P, PIECE], BF16, name="aw%d" % a, tag="aw", align_bytes=64)
-            sg[a] = big.tile([P, PIECE], BF16, name="sg%d" % a, tag="sg", align_bytes=64)
-
-        def mask_rows(a):
+        def stage1(a):
+            wt = stream.tile([P, 2 * K], BF16, name="wt", tag="w", bufs=4)
+            mk = stream.tile([P, 2 * K], BF16, name="mk", tag="m", align_bytes=64)
+            nc.sync.dma_start(out=wt[:], in_=w_view[a])
+            nc.sync.dma_start(out=mk[:], in_=m_view[a])
             for r in range(2):
                 sl = slice(r * K, (r + 1) * K)
-                nc.vector.tensor_tensor(out=wt[a][:, sl], in0=wt[a][:, sl], in1=mk[a][:, sl], op=ALU.mult)
-
-        def mask_pass(a, g):
-            w3 = wt[a][:].rearrange("p (r k) -> p r k", r=2)[:, :, g * 512:(g + 1) * 512]
-            m3 = mk[a][:].rearrange("p (r k) -> p r k", r=2)[:, :, g * 512:(g + 1) * 512]
-            nc.vector.tensor_tensor(out=w3, in0=w3, in1=m3, op=ALU.mult)
-
-        def squares_pe(a):
-            for b in range(DIAG_BLOCKS):
-                for r in range(2):
-                    i_d = (a * DIAG_BLOCKS + b) * 2 + r
-                    blk = wt[a][:, r * K + b * P:r * K + (b + 1) * P]
-                    nc.tensor.matmul(acc_d[:], lhsT=blk, rhs=blk, start=(i_d == 0), stop=(i_d == n_d - 1))
-
-        def squares_act(a):
+                nc.vector.tensor_tensor(out=wt[:, sl], in0=wt[:, sl], in1=mk[:, sl], op=ALU.mult)
+            aw.append(big.tile([P, PIECE], BF16, name="aw%d" % a, tag="aw", align_bytes=64))
+            sg.append(big.tile([P, PIECE], BF16, name="sg%d" % a, tag="sg", align_bytes=64))
+            transpose_rows(wt[:], sg[a][:])
             for r in range(2):
-                junk = stream.tile([P, K - DIAG_BLOCKS * P], BF16, name="junk", tag="junk", bufs=2)
+                for b in range(DIAG_BLOCKS):
+                    i_d = (a * 2 + r) * DIAG_BLOCKS + b
+                    blk = wt[:, r * K + b * P:r * K + (b + 1) * P]
+                    nc.tensor.matmul(acc_d[:], lhsT=blk, rhs=blk, start=(i_d == 0), stop=(i_d == n_d - 1))
+                junk = stream.tile([P, SQ_COLS], BF16, name="junk", tag="junk", bufs=2)
                 nc.scalar.activation(
-                    out=junk[:], in_=wt[a][:, r * K + DIAG_BLOCKS * P:(r + 1) * K], func=ACT.Square,
+                    out=junk[:], in_=wt[:, r * K + DIAG_BLOCKS * P:(r + 1) * K], func=ACT.Square,
                     accum_out=sacc[:, 2 * a + r:2 * a + r + 1],
                 )
 
-        def magnitude(a, lo, hi):
-            sl = slice(lo * 1024, hi * 1024)
-            nc.vector.tensor_single_scalar(out=aw[a][:, sl].bitcast(I32), in_=sg[a][:, sl].bitcast(I32), scalar=0x7FFF7FFF, op=ALU.bitwise_and)
-
-        def sum_magnitude(a, lo, hi):
-            for q in range(lo * 8, hi * 8):
+        def stage2(a):
+            nc.vector.tensor_single_scalar(out=aw[a][:].bitcast(I32), in_=sg[a][:].bitcast(I32), scalar=0x7FFF7FFF, op=ALU.bitwise_and)
+            nc.vector.tensor_scalar(out=sg[a][:], in0=sg[a][:], scalar1=0.0, scalar2=0.5, op0=ALU.is_ge, op1=ALU.subtract)
+            for q in range(32):
                 i_a = a * 32 + q
                 nc.tensor.matmul(acc_a[:], lhsT=aw[a][:, q * P:(q + 1) * P], rhs=ones_b[:, 0:ONES_N], start=(i_a == 0), stop=(i_a == n_a - 1))
 
-        def half_sign(a):
-            nc.vector.tensor_scalar(out=sg[a][:], in0=sg[a][:], scalar1=0.0, scalar2=0.5, op0=ALU.is_ge, op1=ALU.subtract)
+        for a in range(W_LOADS):
+            stage1(a)
+            if a >= 1:
+                stage2(a - 1)
+        stage2(W_LOADS - 1)
 
-        new_piece(0)
-        for g in range(G):
-            mask_pass(0, g)
-            transpose_pass(wt[0][:], sg[0][:], g)
-        squares_pe(0)
-        squares_act(0)
-        for g in range(G):
-            magnitude(0, g, g + 1)
-            sum_magnitude(0, g, g + 1)
-        half_sign(0)
-        load_w(3)
-        new_piece(1)
-        mask_rows(1)
-        for g in range(G):
-            transpose_pass(wt[1][:], sg[1][:], g)
-        squares_pe(1)
-        squares_act(1)
-        for a in range(2, LAST):
-            if a + 2 <= LAST:
-                load_w(a + 2)
-            new_piece(a)
-            mask_rows(a)
-            for g in range(G):
-                transpose_pass(wt[a][:], sg[a][:], g)
-            magnitude(a - 1, 0, G)
-            squares_pe(a)
-            squares_act(a)
-            sum_magnitude(a - 1, 0, G)
-            if a < LAST - 1:
-                half_sign(a - 1)
-
-        xc = const.tile([P, X_LOADS * G * ROWS], U32, name="xc", align_bytes=64)
-        xs = const.tile([P, X_LOADS * G * ROWS], U8, name="xs", align_bytes=64)
-        xt = {}
-        xg = {}
-
-        def load_x(b):
-            xt[b] = stream.tile([P, 2 * K], BF16, name="xt", tag="w", bufs=4)
-            nc.sync.dma_start(out=xt[b][:].rearrange("p (r k) -> p r k", r=2), in_=x_view[b])
-
-        def transpose_x(b, g):
-            if g == 0:
-                xg[b] = stream.tile([P, PIECE], BF16, name="xg", tag="m", align_bytes=64)
-            transpose_pass(xt[b][:], xg[b][:], g)
-
-        def quantise_x(b):
-            sl = slice(b * G * ROWS, (b + 1) * G * ROWS)
-            nc.vector.quantize_mx(out=xc[:, sl].bitcast(FP8X4), scales=xs[:, sl], in_=xg[b][:])
-
-        for b in range(3):
-            load_x(b)
-        new_piece(LAST)
-        for g in range(G):
-            mask_pass(LAST, g)
-            transpose_pass(wt[LAST][:], sg[LAST][:], g)
-        half_sign(LAST - 2)
-        magnitude(LAST - 1, 0, G)
-        squares_pe(LAST)
-        squares_act(LAST)
-        load_x(3)
-        sum_magnitude(LAST - 1, 0, G)
-        for g in range(G):
-            magnitude(LAST, g, g + 1)
-            sum_magnitude(LAST, g, g + 1)
-            if g == 1:
-                half_sign(LAST - 1)
-        half_sign(LAST)
-
-        zd = const.tile([P, P], F32, name="zd")
-        nc.vector.tensor_tensor(out=zd[:], in0=acc_d[:], in1=ident[:], op=ALU.mult)
-        za = const.tile([P, ONES_N], F32, name="za")
-        nc.vector.tensor_copy(out=za[:], in_=acc_a[:])
-        tot = bank(6, [P, P + 2 * W_LOADS])
-        nc.tensor.matmul(tot[:, P:], lhsT=mean_w[:], rhs=sacc[:], start=True, stop=True)
-        transpose_x(0, 0)
-        transpose_x(0, 1)
-        nc.tensor.matmul(tot[:, 0:P], lhsT=mean_w[:], rhs=zd[:], start=True, stop=True)
-        tm = bank(7, [P, ONES_N])
-        nc.tensor.matmul(tm[:], lhsT=mean_w[:], rhs=za[:], start=True, stop=True)
-        transpose_x(0, 2)
-        transpose_x(0, 3)
+        zt = const.tile([P, 2 + P], F32, name="zt")
+        nc.vector.tensor_copy(out=zt[:, 0:2], in_=acc_a[:, 0:2])
+        nc.vector.tensor_tensor(out=zt[:, 2:2 + P], in0=acc_d[:], in1=ident[:], op=ALU.mult)
+        tot = bank(6, [P, 2 + P + 2 * W_LOADS])
+        nc.tensor.matmul(tot[:, 2 + P:], lhsT=mean_w[:], rhs=sacc[:], start=True, stop=True)
+        nc.tensor.matmul(tot[:, 0:2 + P], lhsT=mean_w[:], rhs=zt[:], start=True, stop=True)
         st = const.tile([P, 8], F32, name="st")
-        nc.vector.tensor_reduce(out=st[:, 0:1], in_=tot[:], axis=mybir.AxisListType.X, op=ALU.add)
-        nc.vector.tensor_copy(out=st[:, 1:2], in_=tm[:, 0:1])
+        nc.vector.tensor_reduce(out=st[:, 0:1], in_=tot[:, 2:], axis=mybir.AxisListType.X, op=ALU.add)
+        nc.vector.tensor_copy(out=st[:, 1:2], in_=tot[:, 0:1])
         nc.vector.scalar_tensor_tensor(out=st[:, 2:3], in0=st[:, 1:2], scalar=st[:, 1:2], in1=st[:, 0:1], op0=ALU.mult, op1=ALU.subtract)
-        nc.vector.tensor_scalar(out=st[:, 4:5], in0=st[:, 1:2], scalar1=2.0, scalar2=2e-8, op0=ALU.mult, op1=ALU.add)
         nc.vector.tensor_scalar(out=st[:, 3:4], in0=st[:, 2:3], scalar1=-0.25 * COUNT / (COUNT - 1), scalar2=0.0, op0=ALU.mult, op1=ALU.max)
         thr = const.tile([P, 1], F32, name="thr")
         nc.scalar.activation(out=thr[:], in_=st[:, 3:4], func=ACT.Sqrt)
-        for b in (1, 2):
-            for g in range(G):
-                transpose_x(b, g)
-        quantise_x(0)
-        for g in range(G):
-            transpose_x(3, g)
+        nc.vector.tensor_scalar(out=st[:, 4:5], in0=st[:, 1:2], scalar1=2.0, scalar2=2e-8, op0=ALU.mult, op1=ALU.add)
 
-        wc = {}
-        ws = {}
+        xc = const.tile([P, X_LOADS * G * ROWS], U32, name="xc", align_bytes=64)
+        xs = const.tile([P, X_LOADS * G * ROWS], U8, name="xs", align_bytes=64)
+
+        def load_x(b):
+            xt = stream.tile([P, 2 * K], BF16, name="xt", tag="w", bufs=4)
+            nc.sync.dma_start(out=xt[:], in_=x_view[b])
+            xg = stream.tile([P, PIECE], BF16, name="xg", tag="m", align_bytes=64)
+            transpose_rows(xt[:], xg[:])
+            sl = slice(b * G * ROWS, (b + 1) * G * ROWS)
+            nc.vector.quantize_mx(out=xc[:, sl].bitcast(FP8X4), scales=xs[:, sl], in_=xg[:])
+
+        wc = []
+        ws = []
         accs = {}
-        o_t = {}
-        ots = {}
 
-        def threshold(i):
-            nc.vector.tensor_scalar(out=aw[i][:], in0=aw[i][:], scalar1=thr[:, 0:1], scalar2=st[:, 4:5], op0=ALU.is_gt, op1=ALU.mult)
-
-        def signed(i):
-            nc.vector.tensor_tensor(out=sg[i][:], in0=aw[i][:], in1=sg[i][:], op=ALU.mult)
-
-        def quantise_w(i):
+        def prepare(i):
             if i == 0:
-                wc[i] = const.tile([P, G * ROWS], U32, name="wc0", align_bytes=64)
-                ws[i] = const.tile([P, G * ROWS], U8, name="ws0", align_bytes=64)
+                wc.append(const.tile([P, G * ROWS], U32, name="wc0", align_bytes=64))
+                ws.append(const.tile([P, G * ROWS], U8, name="ws0", align_bytes=64))
             else:
-                wc[i] = big.tile([P, G * ROWS], U32, name="wc%d" % i, tag="aw", align_bytes=64)
-                ws[i] = big.tile([P, G * ROWS], U8, name="ws%d" % i, tag="sg", align_bytes=64)
+                wc.append(big.tile([P, G * ROWS], U32, name="wc%d" % i, tag="aw", align_bytes=64))
+                ws.append(big.tile([P, G * ROWS], U8, name="ws%d" % i, tag="sg", align_bytes=64))
+            nc.vector.tensor_scalar(out=aw[i][:], in0=aw[i][:], scalar1=thr[:, 0:1], scalar2=st[:, 4:5], op0=ALU.is_gt, op1=ALU.mult)
+            nc.vector.tensor_tensor(out=sg[i][:], in0=aw[i][:], in1=sg[i][:], op=ALU.mult)
             nc.vector.quantize_mx(out=wc[i][:].bitcast(FP8X4), scales=ws[i][:], in_=sg[i][:])
 
-        def base(i):
-            return ((i + 1) % 2) * 4
+        def multiply(i):
+            mine = []
+            for b in range(X_LOADS):
+                acc = bank(((i + 1) % 2) * 4 + b, [P, 2 * ROWS])
+                for h in range(2):
+                    for g in range(G):
+                        lo = b * G * ROWS + g * ROWS + h * P
+                        nc.tensor.matmul_mx(
+                            out=acc[:, h * ROWS:(h + 1) * ROWS],
+                            lhsT=xc[:, lo:lo + P].bitcast(FP8X4), lhsT_scale=xs[:, lo:lo + P],
+                            rhs=wc[i][:, g * ROWS:(g + 1) * ROWS].bitcast(FP8X4), rhs_scale=ws[i][:, g * ROWS:(g + 1) * ROWS],
+                            start=(g == 0), stop=(g == G - 1),
+                        )
+                mine.append(acc)
+            accs[i] = mine
 
-        def multiply_n(i, b):
-            acc = bank(base(i) + b, [P, 2 * ROWS])
-            for h in range(2):
-                for g in range(G):
-                    lo = b * G * ROWS + g * ROWS + h * P
-                    nc.tensor.matmul_mx(
-                        out=acc[:, h * ROWS:(h + 1) * ROWS],
-                        lhsT=xc[:, lo:lo + P].bitcast(FP8X4), lhsT_scale=xs[:, lo:lo + P],
-                        rhs=wc[i][:, g * ROWS:(g + 1) * ROWS].bitcast(FP8X4), rhs_scale=ws[i][:, g * ROWS:(g + 1) * ROWS],
-                        start=(g == 0), stop=(g == G - 1),
+        def finish(i):
+            ot = stream.tile([P, 8 * ROWS], F32, name="ot", tag="w", bufs=4)
+            cols = slice(i * ROWS, (i + 1) * ROWS)
+            for b in range(X_LOADS):
+                nc.vector.tensor_tensor(
+                    out=ot[:, b * 2 * ROWS:(b + 1) * 2 * ROWS].rearrange("p (h n) -> p h n", h=2),
+                    in0=accs[i][b][:].rearrange("p (h n) -> p h n", h=2),
+                    in1=bias_bc[:, cols].unsqueeze(1).to_broadcast([P, 2, ROWS]),
+                    op=ALU.add,
+                )
+                if b % 2 == 1:
+                    nc.sync.dma_start(
+                        out=o_view[:, (b - 1) * 2:(b + 1) * 2, cols],
+                        in_=ot[:, (b - 1) * 2 * ROWS:(b + 1) * 2 * ROWS].rearrange("p (i n) -> p i n", i=4),
                     )
-            accs[(i, b)] = acc
 
-        def store(i, q):
-            nc.sync.dma_start(
-                out=o_view[:, (q - 1) * 2:(q + 1) * 2, i * ROWS:(i + 1) * ROWS],
-                in_=ots[i][:, (q - 1) * 2 * ROWS:(q + 1) * 2 * ROWS].rearrange("p (i n) -> p i n", i=4),
-            )
-
-        def finish_n(i, b):
-            if b == 0:
-                ots[i] = stream.tile([P, 8 * ROWS], F32, name="ot", tag="w", bufs=4)
-            nc.vector.tensor_tensor(
-                out=ots[i][:, b * 2 * ROWS:(b + 1) * 2 * ROWS].rearrange("p (h n) -> p h n", h=2),
-                in0=accs[(i, b)][:].rearrange("p (h n) -> p h n", h=2),
-                in1=bias_bc[:, i * ROWS:(i + 1) * ROWS].unsqueeze(1).to_broadcast([P, 2, ROWS]),
-                op=ALU.add,
-            )
-            if b % 2 == 1:
-                store(i, b)
+        o_t = {}
 
         def multiply_t(i):
+            base = ((i + 1) % 2) * 4
             o_t[i] = stream.tile([P, 2 * M], F32, name="o_t", tag="m", align_bytes=64)
             for mh in range(2):
                 for nt in range(2):
-                    acc = bank(base(i) + mh * 2 + nt, [P, 2 * ROWS])
+                    acc = bank(base + mh * 2 + nt, [P, 2 * ROWS])
                     for bb in range(2):
                         for g in range(G):
                             lo = g * ROWS + nt * P
@@ -327,63 +226,43 @@ def tile_masklockedlinear_kernel(tc, x, weight, mask, bias, out):
                     )
 
         def finish_t(i):
-            ots[i] = stream.tile([P, 8 * ROWS], F32, name="ot", tag="w", bufs=4)
+            base = ((i + 1) % 2) * 4
+            ot = stream.tile([P, 8 * ROWS], F32, name="ot", tag="w", bufs=4)
+            cols = slice(i * ROWS, (i + 1) * ROWS)
             for q in range(4):
-                bt = bank(base(i) + q, [P, 2 * ROWS])
+                bt = bank(base + q, [P, 2 * ROWS])
                 for h in range(2):
                     for nt in range(2):
                         mo = nt * M + (2 * q + h) * P
                         nc.tensor.transpose(bt[:, h * ROWS + nt * P:h * ROWS + (nt + 1) * P], o_t[i][:, mo:mo + P], ident[:])
-                nc.scalar.copy(out=ots[i][:, q * 2 * ROWS:(q + 1) * 2 * ROWS], in_=bt[:])
+                nc.scalar.copy(out=ot[:, q * 2 * ROWS:(q + 1) * 2 * ROWS], in_=bt[:])
                 if q % 2 == 1:
-                    store(i, q)
+                    nc.sync.dma_start(
+                        out=o_view[:, (q - 1) * 2:(q + 1) * 2, cols],
+                        in_=ot[:, (q - 1) * 2 * ROWS:(q + 1) * 2 * ROWS].rearrange("p (i n) -> p i n", i=4),
+                    )
 
-        pending = []
-        drained = [0]
-
-        def multiply(i):
+        def mult(i):
             if KINDS[i] == "T":
                 multiply_t(i)
             else:
-                for b in range(X_LOADS):
-                    multiply_n(i, b)
-                    pending.append((i, b))
+                multiply(i)
 
-        def drain(count):
-            for j in range(min(count, len(pending) - drained[0])):
-                i, b = pending[drained[0]]
-                drained[0] += 1
-                finish_n(i, b)
+        def fin(i):
+            if KINDS[i] == "T":
+                finish_t(i)
+            else:
+                finish(i)
 
-        threshold(0)
-        threshold(1)
-        signed(0)
-        quantise_x(1)
-        quantise_w(0)
-        signed(1)
-        multiply_n(0, 0)
-        multiply_n(0, 1)
-        quantise_x(2)
-        quantise_w(1)
-        quantise_x(3)
-        multiply_n(0, 2)
-        multiply_n(0, 3)
+        prepare(0)
         for b in range(X_LOADS):
-            pending.append((0, b))
-        multiply(1)
-        for i in range(2, W_LOADS, 2):
-            threshold(i)
-            drain(1)
-            signed(i)
-            threshold(i + 1)
-            quantise_w(i)
-            drain(1)
-            signed(i + 1)
-            drain(1)
-            quantise_w(i + 1)
-            drain(1)
-            if KINDS[i - 1] == "T":
-                finish_t(i - 1)
-            multiply(i)
-            multiply(i + 1)
-        drain(len(pending))
+            load_x(b)
+        mult(0)
+        prepare(1)
+        mult(1)
+        for i in range(2, W_LOADS):
+            fin(i - 2)
+            prepare(i)
+            mult(i)
+        fin(W_LOADS - 2)
+        fin(W_LOADS - 1)

@@ -18,14 +18,14 @@ P = 128
 M, K, N = 1024, 2048, 2048
 G = K // 512
 ROWS = 256
-W_LOADS = N // ROWS
+PIECES = N // ROWS
 X_LOADS = M // ROWS
 PIECE = G * ROWS * 4
 COUNT = N * K
 DIAG_BLOCKS = 10
-SQ_COLS = K - DIAG_BLOCKS * P
-ONES_N = 8
-KINDS = "TNTTNTTN"
+ONES_N = 2
+T_PIECES = 4
+SCALAR_SIGNS = (0, 6)
 
 
 def tile_masklockedlinear_kernel(tc, x, weight, mask, bias, out):
@@ -33,197 +33,267 @@ def tile_masklockedlinear_kernel(tc, x, weight, mask, bias, out):
     with ExitStack() as ctx:
         const = ctx.enter_context(tc.tile_pool(name="const", bufs=1))
         stream = ctx.enter_context(tc.tile_pool(name="stream", bufs=3))
-        big = ctx.enter_context(tc.tile_pool(name="big", bufs=W_LOADS))
+        big = ctx.enter_context(tc.tile_pool(name="big", bufs=PIECES))
         psum = ctx.enter_context(tc.psum_pool(name="psum", bufs=1))
+        ctx.enter_context(tc.manual_schedule())
 
         def bank(i, shape):
             return psum.tile(shape, F32, name="bank%d" % i, tag="bank%d" % i)
 
-        brow = const.tile([P, N], BF16, name="brow")
-        nc.vector.memset(brow[:], 0.0)
-        nc.sync.dma_start(out=brow[0:1, :], in_=bias.rearrange("(o n) -> o n", o=1))
+        w_view = weight.rearrange("(a p r) k -> a p (r k)", p=P, r=2)
+        m_view = mask.rearrange("(a p r) k -> a p (r k)", p=P, r=2)
+        x_view = x.rearrange("(b r p) k -> b p r k", p=P, r=2)
+        o_view = out.rearrange("(i p) n -> p i n", p=P)
+
+        wts = {}
+        mks = {}
+
+        def load(a, halves):
+            wts[a] = stream.tile([P, 2 * K], BF16, name="wt", tag="w", bufs=4)
+            mks[a] = stream.tile([P, 2 * K], BF16, name="mk", tag="m", align_bytes=64)
+            for c in range(halves):
+                part = slice(c * 2 * K // halves, (c + 1) * 2 * K // halves)
+                nc.sync.dma_start(out=wts[a][:, part], in_=w_view[a][:, part])
+                nc.sync.dma_start(out=mks[a][:, part], in_=m_view[a][:, part])
+
+        load(0, 2)
+        load(1, 2)
+
         ident = const.tile([P, P], F32, name="ident")
         make_identity(nc, ident[:])
+        brow = const.tile([P, (PIECES - T_PIECES) * ROWS], BF16, name="brow")
+        nc.gpsimd.memset(brow[:], 0.0)
         mean_w = const.tile([P, P], F32, name="mean_w")
         nc.vector.memset(mean_w[:], 1.0 / COUNT)
         ones_b = const.tile([P, P], BF16, name="ones_b")
         nc.vector.memset(ones_b[:], 1.0)
+        bsq_b = const.tile([P, ROWS], BF16, name="bsq_b")
+        nc.vector.memset(bsq_b[:], 0.0)
+        bsq = const.tile([P, ROWS], F32, name="bsq")
+        bias_t = const.tile([P, 2 * P], F32, name="bias_t")
+        bias_bc = const.tile([P, (PIECES - T_PIECES) * ROWS], BF16, name="bias_bc")
         warm = const.tile([P, 1], F32, name="warm")
         nc.scalar.activation(out=warm[:], in_=mean_w[:, 0:1], func=ACT.Sqrt)
 
-        w_view = weight.rearrange("(a p r) k -> a p (r k)", p=P, r=2)
-        m_view = mask.rearrange("(a p r) k -> a p (r k)", p=P, r=2)
-        x_view = x.rearrange("(a p r) k -> a p (r k)", p=P, r=2)
-        o_view = out.rearrange("(i p) n -> p i n", p=P)
-
-        def transpose_rows(src, dst):
-            words = src.bitcast(F32)
-            dwords = dst.bitcast(F32)
-            for g in range(G):
-                pt = bank(g, [P, 512])
-                for r in range(2):
-                    for u in range(2):
-                        col = r * 1024 + 256 * g + 128 * u
-                        nc.tensor.transpose(pt[:, (2 * r + u) * P:(2 * r + u + 1) * P], words[:, col:col + P], ident[:])
-                nc.scalar.copy(
-                    out=dwords[:, g * 512:(g + 1) * 512].rearrange("p (j r u) -> p j r u", r=2, u=2),
-                    in_=pt[:].rearrange("p (r u j) -> p j r u", r=2, u=2),
-                )
-
-        bias_bc = const.tile([P, N], BF16, name="bias_bc")
-        for c in range(4):
-            pb = bank(4 + c, [P, 512])
-            nc.tensor.matmul(pb[:], lhsT=ones_b[:], rhs=brow[:, c * 512:(c + 1) * 512], start=True, stop=True)
-            nc.scalar.copy(out=bias_bc[:, c * 512:(c + 1) * 512], in_=pb[:])
-
-        bsq_b = const.tile([P, P], BF16, name="bsq_b")
-        nc.vector.memset(bsq_b[:], 0.0)
-        nc.sync.dma_start(out=bsq_b[0:N // P, :], in_=bias.rearrange("(t n) -> t n", n=P))
-        bsq = const.tile([P, P], F32, name="bsq")
-        nc.vector.tensor_copy(out=bsq[:], in_=bsq_b[:])
-        pq = bank(0, [P, P])
-        nc.tensor.transpose(pq[:], bsq[:], ident[:])
-        bias_t = const.tile([P, N // P], F32, name="bias_t")
-        nc.scalar.copy(out=bias_t[:], in_=pq[:, 0:N // P])
+        nc.sync.dma_start(out=bsq_b[0:PIECES, :], in_=bias.rearrange("(i n) -> i n", n=ROWS))
+        nc.sync.dma_start(out=brow[0:1, :], in_=bias[T_PIECES * ROWS:N].rearrange("(o n) -> o n", o=1))
+        load(2, 1)
 
         acc_a = bank(4, [P, ONES_N])
         acc_d = bank(5, [P, P])
-        sacc = const.tile([P, 2 * W_LOADS], F32, name="sacc")
+        zt = const.tile([P, 2 + 2 * PIECES], F32, name="zt")
         aw = []
         sg = []
-        n_a = W_LOADS * 32
-        n_d = W_LOADS * 2 * DIAG_BLOCKS
-
-        def stage1(a):
-            wt = stream.tile([P, 2 * K], BF16, name="wt", tag="w", bufs=4)
-            mk = stream.tile([P, 2 * K], BF16, name="mk", tag="m", align_bytes=64)
-            nc.sync.dma_start(out=wt[:], in_=w_view[a])
-            nc.sync.dma_start(out=mk[:], in_=m_view[a])
-            for r in range(2):
-                sl = slice(r * K, (r + 1) * K)
-                nc.vector.tensor_tensor(out=wt[:, sl], in0=wt[:, sl], in1=mk[:, sl], op=ALU.mult)
+        for a in range(PIECES):
             aw.append(big.tile([P, PIECE], BF16, name="aw%d" % a, tag="aw", align_bytes=64))
             sg.append(big.tile([P, PIECE], BF16, name="sg%d" % a, tag="sg", align_bytes=64))
-            transpose_rows(wt[:], sg[a][:])
-            for r in range(2):
-                for b in range(DIAG_BLOCKS):
-                    i_d = (a * 2 + r) * DIAG_BLOCKS + b
-                    blk = wt[:, r * K + b * P:r * K + (b + 1) * P]
-                    nc.tensor.matmul(acc_d[:], lhsT=blk, rhs=blk, start=(i_d == 0), stop=(i_d == n_d - 1))
-                junk = stream.tile([P, SQ_COLS], BF16, name="junk", tag="junk", bufs=2)
-                nc.scalar.activation(
-                    out=junk[:], in_=wt[:, r * K + DIAG_BLOCKS * P:(r + 1) * K], func=ACT.Square,
-                    accum_out=sacc[:, 2 * a + r:2 * a + r + 1],
+        n_a = PIECES * 32
+        diag_last = 2 * DIAG_BLOCKS * PIECES - 1
+        diag_done = []
+
+        def mask_row(a, r):
+            sl = slice(r * K, (r + 1) * K)
+            nc.vector.tensor_tensor(out=wts[a][:, sl], in0=wts[a][:, sl], in1=mks[a][:, sl], op=ALU.mult)
+
+        def transpose_row(src, dst, r, first, copies):
+            words = src.bitcast(F32)
+            dwords = dst.bitcast(F32).rearrange("p (g r j u) -> p g r j u", g=G, r=2, u=2)
+            for h in range(2):
+                pt = bank((first + h) % 4, [P, 512])
+                for gg in range(2):
+                    for u in range(2):
+                        col = r * 1024 + 256 * (2 * h + gg) + 128 * u
+                        nc.tensor.transpose(pt[:, (2 * gg + u) * P:(2 * gg + u + 1) * P], words[:, col:col + P], ident[:])
+                copies[h](
+                    out=dwords[:, 2 * h:2 * h + 2, r, :, :],
+                    in_=pt[:].rearrange("p (g u j) -> p g j u", g=2, u=2),
                 )
 
-        def stage2(a):
+        SS = (nc.scalar.copy, nc.scalar.copy)
+        SV = (nc.scalar.copy, nc.vector.tensor_copy)
+
+        def diag(a, r):
+            for b in range(DIAG_BLOCKS):
+                i_d = len(diag_done)
+                diag_done.append(b)
+                blk = wts[a][:, r * K + b * P:r * K + (b + 1) * P]
+                nc.tensor.matmul(acc_d[:], lhsT=blk, rhs=blk, start=(i_d == 0), stop=(i_d == diag_last))
+
+        def squares(a, r):
+            junk = stream.tile([P, K - DIAG_BLOCKS * P], BF16, name="junk", tag="junk", bufs=2)
+            nc.scalar.activation(
+                out=junk[:], in_=wts[a][:, r * K + DIAG_BLOCKS * P:(r + 1) * K], func=ACT.Square,
+                accum_out=zt[:, 2 + 2 * a + r:3 + 2 * a + r],
+            )
+
+        def absolute(a):
             nc.vector.tensor_single_scalar(out=aw[a][:].bitcast(I32), in_=sg[a][:].bitcast(I32), scalar=0x7FFF7FFF, op=ALU.bitwise_and)
-            nc.vector.tensor_scalar(out=sg[a][:], in0=sg[a][:], scalar1=0.0, scalar2=0.5, op0=ALU.is_ge, op1=ALU.subtract)
-            for q in range(32):
-                i_a = a * 32 + q
+
+        def absolute_row(a, r):
+            src = sg[a][:].bitcast(I32).rearrange("p (g r c) -> p g r c", g=G, r=2)
+            dst = aw[a][:].bitcast(I32).rearrange("p (g r c) -> p g r c", g=G, r=2)
+            nc.vector.tensor_single_scalar(out=dst[:, :, r, :], in_=src[:, :, r, :], scalar=0x7FFF7FFF, op=ALU.bitwise_and)
+
+        def sums(a, blocks):
+            for n, q in enumerate(blocks):
+                sums_done.append(q)
+                i_a = len(sums_done) - 1
                 nc.tensor.matmul(acc_a[:], lhsT=aw[a][:, q * P:(q + 1) * P], rhs=ones_b[:, 0:ONES_N], start=(i_a == 0), stop=(i_a == n_a - 1))
 
-        for a in range(W_LOADS):
-            stage1(a)
-            if a >= 1:
-                stage2(a - 1)
-        stage2(W_LOADS - 1)
+        sums_done = []
+        row_blocks = [[q for q in range(32) if (q // 4) % 2 == r] for r in range(2)]
 
-        zt = const.tile([P, 2 + P], F32, name="zt")
-        nc.vector.tensor_copy(out=zt[:, 0:2], in_=acc_a[:, 0:2])
-        nc.vector.tensor_tensor(out=zt[:, 2:2 + P], in0=acc_d[:], in1=ident[:], op=ALU.mult)
-        tot = bank(6, [P, 2 + P + 2 * W_LOADS])
-        nc.tensor.matmul(tot[:, 2 + P:], lhsT=mean_w[:], rhs=sacc[:], start=True, stop=True)
-        nc.tensor.matmul(tot[:, 0:2 + P], lhsT=mean_w[:], rhs=zt[:], start=True, stop=True)
+        def signs_s(a, lo, hi):
+            nc.scalar.activation(out=sg[a][:, lo:hi], in_=sg[a][:, lo:hi], func=ACT.Sign)
+
+        def signs(a, lo, hi):
+            nc.vector.tensor_scalar(out=sg[a][:, lo:hi], in0=sg[a][:, lo:hi], scalar1=0.0, scalar2=0.5, op0=ALU.is_ge, op1=ALU.subtract)
+
+        def spread_bias():
+            nc.vector.tensor_copy(out=bsq[:], in_=bsq_b[:])
+            pq = bank(6, [P, 2 * P])
+            for r in range(2):
+                nc.tensor.transpose(pq[:, r * P:(r + 1) * P], bsq[:].rearrange("p (j r) -> p r j", r=2)[:, r, :], ident[:])
+            nc.scalar.copy(out=bias_t[:], in_=pq[:])
+            width = (PIECES - T_PIECES) * ROWS
+            for c in range(0, width, 512):
+                w = min(512, width - c)
+                pb = bank(6 + (c // 512 + 1) % 2, [P, w])
+                nc.tensor.matmul(pb[:], lhsT=ones_b[:], rhs=brow[:, c:c + w], start=True, stop=True)
+                nc.scalar.copy(out=bias_bc[:, c:c + w], in_=pb[:])
+
+        for a in range(PIECES - 1):
+            mask_row(a, 0)
+            mask_row(a, 1)
+            for r in range(2):
+                transpose_row(wts[a][:], sg[a][:], r, 2 * r, SS)
+                diag(a, r)
+                squares(a, r)
+            if a >= 1:
+                absolute(a - 1)
+                sums(a - 1, range(32))
+            if 2 <= a < 5:
+                signs(a - 1, 0, PIECE)
+            if 1 <= a < 4:
+                signs_s(0, (0, 0, 2, 3)[a] * PIECE // 4, (0, 2, 3, 4)[a] * PIECE // 4)
+            if a == 2:
+                spread_bias()
+            if a + 3 < PIECES:
+                load(a + 3, 2 if a + 3 == PIECES - 1 else 1)
+
+        xc = const.tile([P, G * M], U32, name="xc", align_bytes=64)
+        xs = const.tile([P, G * M], U8, name="xs", align_bytes=64)
+        xts = {}
+        xgs = {}
+
+        def load_x(b):
+            xts[b] = stream.tile([P, 2 * K], BF16, name="xt", tag="w", bufs=4)
+            nc.sync.dma_start(out=xts[b][:].rearrange("p (r k) -> p r k", r=2), in_=x_view[b])
+
+        def transpose_x(b):
+            xgs[b] = stream.tile([P, PIECE], BF16, name="xg", tag="m", align_bytes=64)
+            for r in range(2):
+                transpose_row(xts[b][:], xgs[b][:], r, 2 * r, SS)
+
+        def quantise_x(b, passes):
+            for g in passes:
+                lo = g * M + b * ROWS
+                nc.vector.quantize_mx(
+                    out=xc[:, lo:lo + ROWS].bitcast(FP8X4), scales=xs[:, lo:lo + ROWS],
+                    in_=xgs[b][:, g * 4 * ROWS:(g + 1) * 4 * ROWS],
+                )
+
+        load_x(0)
+        load_x(1)
+        load_x(2)
+        a = PIECES - 1
+        HALF = PIECE // 2
+        mask_row(a, 0)
+        diag(a, 0)
+        squares(a, 0)
+        mask_row(a, 1)
+        squares(a, 1)
+        absn = const.tile([P, 2 * K], BF16, name="absn")
+        nc.vector.tensor_single_scalar(out=absn[:].bitcast(I32), in_=wts[a][:].bitcast(I32), scalar=0x7FFF7FFF, op=ALU.bitwise_and)
+        absolute(a - 1)
+        diag(a, 1)
+        xgs[0] = stream.tile([P, PIECE], BF16, name="xg", tag="m", align_bytes=64)
+        transpose_row(xts[0][:], xgs[0][:], 0, 0, SS)
+        for q in range(32):
+            nc.tensor.matmul(acc_a[:], lhsT=absn[:, q * P:(q + 1) * P], rhs=ones_b[:, 0:ONES_N], start=False, stop=False)
+        sums_done.extend(range(32))
+        sums(a - 1, range(32))
+
         st = const.tile([P, 8], F32, name="st")
-        nc.vector.tensor_reduce(out=st[:, 0:1], in_=tot[:, 2:], axis=mybir.AxisListType.X, op=ALU.add)
+        thr = const.tile([P, 1], F32, name="thr")
+        dj = const.tile([P, P], F32, name="dj")
+        nc.vector.scalar_tensor_tensor(out=dj[:], in0=acc_d[:], scalar=1.0, in1=ident[:], op0=ALU.mult, op1=ALU.mult, accum_out=zt[:, 1:2])
+        nc.vector.tensor_copy(out=zt[:, 0:1], in_=acc_a[:, 0:1])
+        tot = bank(6, [P, 2 + 2 * PIECES])
+        nc.tensor.matmul(tot[:], lhsT=mean_w[:], rhs=zt[:], start=True, stop=True)
+        signs(a - 3, 0, HALF)
+        nc.vector.tensor_reduce(out=st[:, 0:1], in_=tot[:, 1:], axis=mybir.AxisListType.X, op=ALU.add)
         nc.vector.tensor_copy(out=st[:, 1:2], in_=tot[:, 0:1])
         nc.vector.scalar_tensor_tensor(out=st[:, 2:3], in0=st[:, 1:2], scalar=st[:, 1:2], in1=st[:, 0:1], op0=ALU.mult, op1=ALU.subtract)
         nc.vector.tensor_scalar(out=st[:, 3:4], in0=st[:, 2:3], scalar1=-0.25 * COUNT / (COUNT - 1), scalar2=0.0, op0=ALU.mult, op1=ALU.max)
-        thr = const.tile([P, 1], F32, name="thr")
         nc.scalar.activation(out=thr[:], in_=st[:, 3:4], func=ACT.Sqrt)
         nc.vector.tensor_scalar(out=st[:, 4:5], in0=st[:, 1:2], scalar1=2.0, scalar2=2e-8, op0=ALU.mult, op1=ALU.add)
+        nc.vector.tensor_scalar(out=st[:, 5:6], in0=st[:, 1:2], scalar1=1.0, scalar2=1e-8, op0=ALU.mult, op1=ALU.add)
+        signs(a - 3, HALF, PIECE)
 
-        xc = const.tile([P, X_LOADS * G * ROWS], U32, name="xc", align_bytes=64)
-        xs = const.tile([P, X_LOADS * G * ROWS], U8, name="xs", align_bytes=64)
-
-        def load_x(b):
-            xt = stream.tile([P, 2 * K], BF16, name="xt", tag="w", bufs=4)
-            nc.sync.dma_start(out=xt[:], in_=x_view[b])
-            xg = stream.tile([P, PIECE], BF16, name="xg", tag="m", align_bytes=64)
-            transpose_rows(xt[:], xg[:])
-            sl = slice(b * G * ROWS, (b + 1) * G * ROWS)
-            nc.vector.quantize_mx(out=xc[:, sl].bitcast(FP8X4), scales=xs[:, sl], in_=xg[:])
-
-        wc = []
-        ws = []
+        wc = {}
+        ws = {}
         accs = {}
-
-        def prepare(i):
-            if i == 0:
-                wc.append(const.tile([P, G * ROWS], U32, name="wc0", align_bytes=64))
-                ws.append(const.tile([P, G * ROWS], U8, name="ws0", align_bytes=64))
-            else:
-                wc.append(big.tile([P, G * ROWS], U32, name="wc%d" % i, tag="aw", align_bytes=64))
-                ws.append(big.tile([P, G * ROWS], U8, name="ws%d" % i, tag="sg", align_bytes=64))
-            nc.vector.tensor_scalar(out=aw[i][:], in0=aw[i][:], scalar1=thr[:, 0:1], scalar2=st[:, 4:5], op0=ALU.is_gt, op1=ALU.mult)
-            nc.vector.tensor_tensor(out=sg[i][:], in0=aw[i][:], in1=sg[i][:], op=ALU.mult)
-            nc.vector.quantize_mx(out=wc[i][:].bitcast(FP8X4), scales=ws[i][:], in_=sg[i][:])
-
-        def multiply(i):
-            mine = []
-            for b in range(X_LOADS):
-                acc = bank(((i + 1) % 2) * 4 + b, [P, 2 * ROWS])
-                for h in range(2):
-                    for g in range(G):
-                        lo = b * G * ROWS + g * ROWS + h * P
-                        nc.tensor.matmul_mx(
-                            out=acc[:, h * ROWS:(h + 1) * ROWS],
-                            lhsT=xc[:, lo:lo + P].bitcast(FP8X4), lhsT_scale=xs[:, lo:lo + P],
-                            rhs=wc[i][:, g * ROWS:(g + 1) * ROWS].bitcast(FP8X4), rhs_scale=ws[i][:, g * ROWS:(g + 1) * ROWS],
-                            start=(g == 0), stop=(g == G - 1),
-                        )
-                mine.append(acc)
-            accs[i] = mine
-
-        def finish(i):
-            ot = stream.tile([P, 8 * ROWS], F32, name="ot", tag="w", bufs=4)
-            cols = slice(i * ROWS, (i + 1) * ROWS)
-            for b in range(X_LOADS):
-                nc.vector.tensor_tensor(
-                    out=ot[:, b * 2 * ROWS:(b + 1) * 2 * ROWS].rearrange("p (h n) -> p h n", h=2),
-                    in0=accs[i][b][:].rearrange("p (h n) -> p h n", h=2),
-                    in1=bias_bc[:, cols].unsqueeze(1).to_broadcast([P, 2, ROWS]),
-                    op=ALU.add,
-                )
-                if b % 2 == 1:
-                    nc.sync.dma_start(
-                        out=o_view[:, (b - 1) * 2:(b + 1) * 2, cols],
-                        in_=ot[:, (b - 1) * 2 * ROWS:(b + 1) * 2 * ROWS].rearrange("p (i n) -> p i n", i=4),
-                    )
-
         o_t = {}
 
-        def multiply_t(i):
+        def tern_abs(i, lo, hi):
+            nc.vector.tensor_scalar(out=aw[i][:, lo:hi], in0=aw[i][:, lo:hi], scalar1=thr[:, 0:1], scalar2=st[:, 5:6] if i in SCALAR_SIGNS else st[:, 4:5], op0=ALU.is_gt, op1=ALU.mult)
+
+        def tern_sign(i, lo, hi):
+            nc.vector.tensor_tensor(out=sg[i][:, lo:hi], in0=aw[i][:, lo:hi], in1=sg[i][:, lo:hi], op=ALU.mult)
+
+        def codes(i):
+            if i == 0:
+                wc[i] = const.tile([P, G * ROWS], U32, name="wc0", align_bytes=64)
+                ws[i] = const.tile([P, G * ROWS], U8, name="ws0", align_bytes=64)
+            else:
+                wc[i] = big.tile([P, G * ROWS], U32, name="wc%d" % i, tag="aw", align_bytes=64)
+                ws[i] = big.tile([P, G * ROWS], U8, name="ws%d" % i, tag="sg", align_bytes=64)
+
+        def quantise_w(i, lo, hi):
+            nc.vector.quantize_mx(out=wc[i][:, lo // 4:hi // 4].bitcast(FP8X4), scales=ws[i][:, lo // 4:hi // 4], in_=sg[i][:, lo:hi])
+
+        def pass_t(i, acc, mh, nt, g):
+            lo = g * ROWS + nt * P
+            xo = g * M + mh * 512
+            nc.tensor.matmul_mx(
+                out=acc[:], lhsT=wc[i][:, lo:lo + P].bitcast(FP8X4), lhsT_scale=ws[i][:, lo:lo + P],
+                rhs=xc[:, xo:xo + 512].bitcast(FP8X4), rhs_scale=xs[:, xo:xo + 512],
+                start=(g == 0), stop=(g == G - 1),
+            )
+
+        def out_t(i, acc, mh, nt):
+            nc.scalar.activation(
+                out=o_t[i][:, nt * M + mh * 512:nt * M + (mh + 1) * 512], in_=acc[:], func=ACT.Identity,
+                bias=bias_t[:, nt * P + i:nt * P + i + 1], scale=1.0,
+            )
+
+        def multiply_t(i, mh):
             base = ((i + 1) % 2) * 4
-            o_t[i] = stream.tile([P, 2 * M], F32, name="o_t", tag="m", align_bytes=64)
-            for mh in range(2):
+            if mh == 0:
+                o_t[i] = stream.tile([P, 2 * M], F32, name="o_t", tag="m", align_bytes=64)
+            pair = [bank(base + mh * 2 + nt, [P, 512]) for nt in range(2)]
+            if i == 0:
+                for g in range(G):
+                    for nt in range(2):
+                        pass_t(i, pair[nt], mh, nt, g)
                 for nt in range(2):
-                    acc = bank(base + mh * 2 + nt, [P, 2 * ROWS])
-                    for bb in range(2):
-                        for g in range(G):
-                            lo = g * ROWS + nt * P
-                            xo = (mh * 2 + bb) * G * ROWS + g * ROWS
-                            nc.tensor.matmul_mx(
-                                out=acc[:, bb * ROWS:(bb + 1) * ROWS],
-                                lhsT=wc[i][:, lo:lo + P].bitcast(FP8X4), lhsT_scale=ws[i][:, lo:lo + P],
-                                rhs=xc[:, xo:xo + ROWS].bitcast(FP8X4), rhs_scale=xs[:, xo:xo + ROWS],
-                                start=(g == 0), stop=(g == G - 1),
-                            )
-                    nc.scalar.activation(
-                        out=o_t[i][:, nt * M + mh * 512:nt * M + (mh + 1) * 512], in_=acc[:], func=ACT.Identity,
-                        bias=bias_t[:, 2 * i + nt:2 * i + nt + 1], scale=1.0,
-                    )
+                    out_t(i, pair[nt], mh, nt)
+            else:
+                for nt in range(2):
+                    for g in range(G):
+                        pass_t(i, pair[nt], mh, nt, g)
+                    out_t(i, pair[nt], mh, nt)
 
         def finish_t(i):
             base = ((i + 1) % 2) * 4
@@ -235,34 +305,104 @@ def tile_masklockedlinear_kernel(tc, x, weight, mask, bias, out):
                     for nt in range(2):
                         mo = nt * M + (2 * q + h) * P
                         nc.tensor.transpose(bt[:, h * ROWS + nt * P:h * ROWS + (nt + 1) * P], o_t[i][:, mo:mo + P], ident[:])
-                nc.scalar.copy(out=ot[:, q * 2 * ROWS:(q + 1) * 2 * ROWS], in_=bt[:])
+                nc.scalar.copy(
+                    out=ot[:, q * 2 * ROWS:(q + 1) * 2 * ROWS].rearrange("p (h j r) -> p h j r", h=2, r=2),
+                    in_=bt[:].rearrange("p (h r j) -> p h j r", h=2, r=2),
+                )
                 if q % 2 == 1:
                     nc.sync.dma_start(
                         out=o_view[:, (q - 1) * 2:(q + 1) * 2, cols],
                         in_=ot[:, (q - 1) * 2 * ROWS:(q + 1) * 2 * ROWS].rearrange("p (i n) -> p i n", i=4),
                     )
 
-        def mult(i):
-            if KINDS[i] == "T":
-                multiply_t(i)
-            else:
-                multiply(i)
+        def multiply_n(i):
+            accs[i] = []
+            for q in range(4):
+                acc = bank(((i + 1) % 2) * 4 + q, [P, 2 * ROWS])
+                for h in range(2):
+                    for g in range(G):
+                        lo = g * M + (2 * q + h) * P
+                        nc.tensor.matmul_mx(
+                            out=acc[:, h * ROWS:(h + 1) * ROWS],
+                            lhsT=xc[:, lo:lo + P].bitcast(FP8X4), lhsT_scale=xs[:, lo:lo + P],
+                            rhs=wc[i][:, g * ROWS:(g + 1) * ROWS].bitcast(FP8X4), rhs_scale=ws[i][:, g * ROWS:(g + 1) * ROWS],
+                            start=(g == 0), stop=(g == G - 1),
+                        )
+                accs[i].append(acc)
 
-        def fin(i):
-            if KINDS[i] == "T":
-                finish_t(i)
-            else:
-                finish(i)
+        def finish_n(i):
+            ot = stream.tile([P, 8 * ROWS], F32, name="ot", tag="w", bufs=4)
+            cols = slice(i * ROWS, (i + 1) * ROWS)
+            bcols = slice((i - T_PIECES) * ROWS, (i - T_PIECES + 1) * ROWS)
+            for q in range(4):
+                nc.vector.tensor_tensor(
+                    out=ot[:, q * 2 * ROWS:(q + 1) * 2 * ROWS].rearrange("p (h j r) -> p h j r", h=2, r=2),
+                    in0=accs[i][q][:].rearrange("p (h r j) -> p h j r", h=2, r=2),
+                    in1=bias_bc[:, bcols].rearrange("p (j r) -> p j r", r=2).unsqueeze(1).to_broadcast([P, 2, P, 2]),
+                    op=ALU.add,
+                )
+                nc.sync.dma_start(
+                    out=o_view[:, q * 2:(q + 1) * 2, cols],
+                    in_=ot[:, q * 2 * ROWS:(q + 1) * 2 * ROWS].rearrange("p (i n) -> p i n", i=2),
+                )
 
-        prepare(0)
-        for b in range(X_LOADS):
-            load_x(b)
-        mult(0)
-        prepare(1)
-        mult(1)
-        for i in range(2, W_LOADS):
-            fin(i - 2)
-            prepare(i)
-            mult(i)
-        fin(W_LOADS - 2)
-        fin(W_LOADS - 1)
+        Q = PIECE // G
+        transpose_row(xts[0][:], xgs[0][:], 1, 2, SS)
+        transpose_x(1)
+        codes(0)
+        tern_abs(0, 0, Q)
+        tern_abs(0, Q, 2 * Q)
+        tern_sign(0, 0, Q)
+        tern_abs(0, 2 * Q, 3 * Q)
+        tern_sign(0, Q, 2 * Q)
+        quantise_w(0, 0, Q)
+        quantise_x(0, range(G))
+        tern_abs(0, 3 * Q, 4 * Q)
+        tern_sign(0, 2 * Q, 3 * Q)
+        quantise_w(0, Q, 2 * Q)
+        quantise_x(1, range(G))
+        tern_sign(0, 3 * Q, 4 * Q)
+        quantise_w(0, 2 * Q, 3 * Q)
+        load_x(3)
+        transpose_x(2)
+        transpose_x(3)
+        quantise_x(2, range(G))
+        quantise_w(0, 3 * Q, 4 * Q)
+        multiply_t(0, 0)
+        tern_abs(1, 0, PIECE)
+        quantise_x(3, range(G))
+        tern_sign(1, 0, PIECE)
+        tern_abs(2, 0, PIECE)
+        codes(1)
+        quantise_w(1, 0, PIECE)
+        multiply_t(0, 1)
+        transpose_row(wts[a][:], sg[a][:], 0, 0, SS)
+        transpose_row(wts[a][:], sg[a][:], 1, 2, SS)
+        signs_s(6, 0, PIECE // 4)
+        multiply_t(1, 0)
+        multiply_t(1, 1)
+        finish_t(0)
+        for i in range(2, PIECES):
+            if i == 3:
+                signs(5, 0, PIECE)
+            if i == 5:
+                absolute(a)
+                signs(a, 0, PIECE)
+            if i < 5:
+                signs_s(6, (i - 1) * PIECE // 4, i * PIECE // 4)
+            tern_sign(i, 0, PIECE)
+            if i + 1 < PIECES:
+                tern_abs(i + 1, 0, PIECE)
+            codes(i)
+            quantise_w(i, 0, PIECE)
+            if i - 2 >= T_PIECES:
+                finish_n(i - 2)
+            if i < T_PIECES:
+                multiply_t(i, 0)
+                multiply_t(i, 1)
+            else:
+                multiply_n(i)
+            if i - 1 < T_PIECES:
+                finish_t(i - 1)
+        finish_n(PIECES - 2)
+        finish_n(PIECES - 1)

@@ -25,7 +25,7 @@ COUNT = N * K
 DIAG_BLOCKS = 10
 ONES_N = 2
 T_PIECES = 4
-SCALAR_SIGNS = (0, 6)
+SCALAR_SIGNS = ()
 
 
 def tile_masklockedlinear_kernel(tc, x, weight, mask, bias, out):
@@ -48,16 +48,16 @@ def tile_masklockedlinear_kernel(tc, x, weight, mask, bias, out):
         wts = {}
         mks = {}
 
-        def load(a, halves):
+        def load(a, cuts):
             wts[a] = stream.tile([P, 2 * K], BF16, name="wt", tag="w", bufs=4)
             mks[a] = stream.tile([P, 2 * K], BF16, name="mk", tag="m", align_bytes=64)
-            for c in range(halves):
-                part = slice(c * 2 * K // halves, (c + 1) * 2 * K // halves)
+            for lo, hi in zip((0,) + cuts, cuts + (2 * K,)):
+                part = slice(lo, hi)
                 nc.sync.dma_start(out=wts[a][:, part], in_=w_view[a][:, part])
-                nc.sync.dma_start(out=mks[a][:, part], in_=m_view[a][:, part])
+                nc.scalar.dma_start(out=mks[a][:, part], in_=m_view[a][:, part])
 
-        load(0, 2)
-        load(1, 2)
+        load(0, (K,))
+        load(1, (K,))
 
         ident = const.tile([P, P], F32, name="ident")
         make_identity(nc, ident[:])
@@ -77,22 +77,25 @@ def tile_masklockedlinear_kernel(tc, x, weight, mask, bias, out):
 
         nc.sync.dma_start(out=bsq_b[0:PIECES, :], in_=bias.rearrange("(i n) -> i n", n=ROWS))
         nc.sync.dma_start(out=brow[0:1, :], in_=bias[T_PIECES * ROWS:N].rearrange("(o n) -> o n", o=1))
-        load(2, 1)
+        load(2, ())
 
         acc_a = bank(4, [P, ONES_N])
         acc_d = bank(5, [P, P])
-        zt = const.tile([P, 2 + 2 * PIECES], F32, name="zt")
+        zt = const.tile([P, 1 + 2 * PIECES], F32, name="zt")
         aw = []
         sg = []
         for a in range(PIECES):
             aw.append(big.tile([P, PIECE], BF16, name="aw%d" % a, tag="aw", align_bytes=64))
             sg.append(big.tile([P, PIECE], BF16, name="sg%d" % a, tag="sg", align_bytes=64))
         n_a = PIECES * 32
-        diag_last = 2 * DIAG_BLOCKS * PIECES - 1
+        diag_last = DIAG_BLOCKS * (2 * PIECES - 1) + 16 - 1
         diag_done = []
 
         def mask_row(a, r):
-            sl = slice(r * K, (r + 1) * K)
+            mask_cols(a, r * K, (r + 1) * K)
+
+        def mask_cols(a, lo, hi):
+            sl = slice(lo, hi)
             nc.vector.tensor_tensor(out=wts[a][:, sl], in0=wts[a][:, sl], in1=mks[a][:, sl], op=ALU.mult)
 
         def transpose_row(src, dst, r, first, copies):
@@ -112,8 +115,8 @@ def tile_masklockedlinear_kernel(tc, x, weight, mask, bias, out):
         SS = (nc.scalar.copy, nc.scalar.copy)
         SV = (nc.scalar.copy, nc.vector.tensor_copy)
 
-        def diag(a, r):
-            for b in range(DIAG_BLOCKS):
+        def diag(a, r, blocks=range(DIAG_BLOCKS)):
+            for b in blocks:
                 i_d = len(diag_done)
                 diag_done.append(b)
                 blk = wts[a][:, r * K + b * P:r * K + (b + 1) * P]
@@ -165,21 +168,20 @@ def tile_masklockedlinear_kernel(tc, x, weight, mask, bias, out):
         for a in range(PIECES - 1):
             mask_row(a, 0)
             mask_row(a, 1)
+            if a >= 1:
+                absolute(a - 1)
             for r in range(2):
                 transpose_row(wts[a][:], sg[a][:], r, 2 * r, SS)
                 diag(a, r)
                 squares(a, r)
             if a >= 1:
-                absolute(a - 1)
                 sums(a - 1, range(32))
-            if 2 <= a < 5:
+            if 1 <= a < 6:
                 signs(a - 1, 0, PIECE)
-            if 1 <= a < 4:
-                signs_s(0, (0, 0, 2, 3)[a] * PIECE // 4, (0, 2, 3, 4)[a] * PIECE // 4)
             if a == 2:
                 spread_bias()
             if a + 3 < PIECES:
-                load(a + 3, 2 if a + 3 == PIECES - 1 else 1)
+                load(a + 3, (K, K + K // 2) if a + 3 == PIECES - 1 else ())
 
         xc = const.tile([P, G * M], U32, name="xc", align_bytes=64)
         xs = const.tile([P, G * M], U8, name="xs", align_bytes=64)
@@ -208,38 +210,52 @@ def tile_masklockedlinear_kernel(tc, x, weight, mask, bias, out):
         load_x(2)
         a = PIECES - 1
         HALF = PIECE // 2
+        absn = const.tile([P, 2 * K], BF16, name="absn")
+
+        def absolute_cols(lo, hi):
+            nc.vector.tensor_single_scalar(out=absn[:, lo:hi].bitcast(I32), in_=wts[a][:, lo:hi].bitcast(I32), scalar=0x7FFF7FFF, op=ALU.bitwise_and)
+
+        def sums_cols(lo, hi):
+            for q in range(lo // P, hi // P):
+                sums_done.append(q)
+                nc.tensor.matmul(acc_a[:], lhsT=absn[:, q * P:(q + 1) * P], rhs=ones_b[:, 0:ONES_N], start=False, stop=(len(sums_done) == n_a))
+
         mask_row(a, 0)
         diag(a, 0)
         squares(a, 0)
-        mask_row(a, 1)
-        squares(a, 1)
-        absn = const.tile([P, 2 * K], BF16, name="absn")
-        nc.vector.tensor_single_scalar(out=absn[:].bitcast(I32), in_=wts[a][:].bitcast(I32), scalar=0x7FFF7FFF, op=ALU.bitwise_and)
         absolute(a - 1)
-        diag(a, 1)
-        xgs[0] = stream.tile([P, PIECE], BF16, name="xg", tag="m", align_bytes=64)
-        transpose_row(xts[0][:], xgs[0][:], 0, 0, SS)
-        for q in range(32):
-            nc.tensor.matmul(acc_a[:], lhsT=absn[:, q * P:(q + 1) * P], rhs=ones_b[:, 0:ONES_N], start=False, stop=False)
-        sums_done.extend(range(32))
         sums(a - 1, range(32))
+        absolute_cols(0, K)
+        sums_cols(0, K)
+        load_x(3)
+        for c in range(2):
+            lo = K + c * K // 2
+            mask_cols(a, lo, lo + K // 2)
+            diag(a, 1, range(8 * c, 8 * c + 8))
+            absolute_cols(lo, lo + K // 2)
+            sums_cols(lo, lo + K // 2)
+            if c == 0:
+                xgs[0] = stream.tile([P, PIECE], BF16, name="xg", tag="m", align_bytes=64)
 
+        EIGHTH = PIECE // 8
+        signs(a - 2, 0, 2 * EIGHTH)
         st = const.tile([P, 8], F32, name="st")
         thr = const.tile([P, 1], F32, name="thr")
         dj = const.tile([P, P], F32, name="dj")
         nc.vector.scalar_tensor_tensor(out=dj[:], in0=acc_d[:], scalar=1.0, in1=ident[:], op0=ALU.mult, op1=ALU.mult, accum_out=zt[:, 1:2])
         nc.vector.tensor_copy(out=zt[:, 0:1], in_=acc_a[:, 0:1])
-        tot = bank(6, [P, 2 + 2 * PIECES])
+        tot = bank(6, [P, 1 + 2 * PIECES])
         nc.tensor.matmul(tot[:], lhsT=mean_w[:], rhs=zt[:], start=True, stop=True)
-        signs(a - 3, 0, HALF)
+        signs(a - 2, 2 * EIGHTH, 4 * EIGHTH)
         nc.vector.tensor_reduce(out=st[:, 0:1], in_=tot[:, 1:], axis=mybir.AxisListType.X, op=ALU.add)
         nc.vector.tensor_copy(out=st[:, 1:2], in_=tot[:, 0:1])
+        signs(a - 2, 4 * EIGHTH, 5 * EIGHTH)
         nc.vector.scalar_tensor_tensor(out=st[:, 2:3], in0=st[:, 1:2], scalar=st[:, 1:2], in1=st[:, 0:1], op0=ALU.mult, op1=ALU.subtract)
         nc.vector.tensor_scalar(out=st[:, 3:4], in0=st[:, 2:3], scalar1=-0.25 * COUNT / (COUNT - 1), scalar2=0.0, op0=ALU.mult, op1=ALU.max)
         nc.scalar.activation(out=thr[:], in_=st[:, 3:4], func=ACT.Sqrt)
+        signs(a - 2, 5 * EIGHTH, PIECE)
         nc.vector.tensor_scalar(out=st[:, 4:5], in0=st[:, 1:2], scalar1=2.0, scalar2=2e-8, op0=ALU.mult, op1=ALU.add)
         nc.vector.tensor_scalar(out=st[:, 5:6], in0=st[:, 1:2], scalar1=1.0, scalar2=1e-8, op0=ALU.mult, op1=ALU.add)
-        signs(a - 3, HALF, PIECE)
 
         wc = {}
         ws = {}
@@ -272,6 +288,13 @@ def tile_masklockedlinear_kernel(tc, x, weight, mask, bias, out):
                 start=(g == 0), stop=(g == G - 1),
             )
 
+        sign_queue = [(s, c) for s in SCALAR_SIGNS for c in range(8)]
+
+        def sign_some(count):
+            for c in range(min(count, len(sign_queue))):
+                s, c = sign_queue.pop(0)
+                signs_s(s, c * EIGHTH, (c + 1) * EIGHTH)
+
         def out_t(i, acc, mh, nt):
             nc.scalar.activation(
                 out=o_t[i][:, nt * M + mh * 512:nt * M + (mh + 1) * 512], in_=acc[:], func=ACT.Identity,
@@ -294,6 +317,8 @@ def tile_masklockedlinear_kernel(tc, x, weight, mask, bias, out):
                     for g in range(G):
                         pass_t(i, pair[nt], mh, nt, g)
                     out_t(i, pair[nt], mh, nt)
+                    if i < T_PIECES - 1 and (mh, nt) != (1, 1):
+                        sign_some(1)
 
         def finish_t(i):
             base = ((i + 1) % 2) * 4
@@ -347,6 +372,7 @@ def tile_masklockedlinear_kernel(tc, x, weight, mask, bias, out):
                 )
 
         Q = PIECE // G
+        transpose_row(xts[0][:], xgs[0][:], 0, 0, SS)
         transpose_row(xts[0][:], xgs[0][:], 1, 2, SS)
         transpose_x(1)
         codes(0)
@@ -363,33 +389,31 @@ def tile_masklockedlinear_kernel(tc, x, weight, mask, bias, out):
         quantise_x(1, range(G))
         tern_sign(0, 3 * Q, 4 * Q)
         quantise_w(0, 2 * Q, 3 * Q)
-        load_x(3)
         transpose_x(2)
         transpose_x(3)
         quantise_x(2, range(G))
         quantise_w(0, 3 * Q, 4 * Q)
+        sign_some(2)
         multiply_t(0, 0)
+        sign_some(2)
         tern_abs(1, 0, PIECE)
         quantise_x(3, range(G))
         tern_sign(1, 0, PIECE)
-        tern_abs(2, 0, PIECE)
         codes(1)
         quantise_w(1, 0, PIECE)
+        tern_abs(2, 0, PIECE)
         multiply_t(0, 1)
         transpose_row(wts[a][:], sg[a][:], 0, 0, SS)
         transpose_row(wts[a][:], sg[a][:], 1, 2, SS)
-        signs_s(6, 0, PIECE // 4)
         multiply_t(1, 0)
         multiply_t(1, 1)
         finish_t(0)
         for i in range(2, PIECES):
-            if i == 3:
-                signs(5, 0, PIECE)
             if i == 5:
+                signs(6, 0, PIECE)
+            if i == 6:
                 absolute(a)
                 signs(a, 0, PIECE)
-            if i < 5:
-                signs_s(6, (i - 1) * PIECE // 4, i * PIECE // 4)
             tern_sign(i, 0, PIECE)
             if i + 1 < PIECES:
                 tern_abs(i + 1, 0, PIECE)
@@ -404,5 +428,7 @@ def tile_masklockedlinear_kernel(tc, x, weight, mask, bias, out):
                 multiply_n(i)
             if i - 1 < T_PIECES:
                 finish_t(i - 1)
+            if i == T_PIECES - 1:
+                sign_some(len(sign_queue))
         finish_n(PIECES - 2)
         finish_n(PIECES - 1)

@@ -54,7 +54,7 @@ def tile_masklockedlinear_kernel(tc, x, weight, mask, bias, out):
             for lo, hi in zip((0,) + cuts, cuts + (2 * K,)):
                 part = slice(lo, hi)
                 nc.sync.dma_start(out=wts[a][:, part], in_=w_view[a][:, part])
-                nc.scalar.dma_start(out=mks[a][:, part], in_=m_view[a][:, part])
+                nc.sync.dma_start(out=mks[a][:, part], in_=m_view[a][:, part])
 
         load(0, (K,))
         load(1, (K,))

@@ -23,9 +23,9 @@ X_LOADS = M // ROWS
 PIECE = G * ROWS * 4
 COUNT = N * K
 DIAG_BLOCKS = 10
-ONES_N = 2
+ONES_N = 14
 T_PIECES = 4
-SCALAR_SIGNS = ()
+SCALAR_SIGNS = (6, )
 
 
 def tile_masklockedlinear_kernel(tc, x, weight, mask, bias, out):
@@ -176,12 +176,12 @@ def tile_masklockedlinear_kernel(tc, x, weight, mask, bias, out):
                 squares(a, r)
             if a >= 1:
                 sums(a - 1, range(32))
-            if 1 <= a < 6:
+            if 1 <= a < 5:
                 signs(a - 1, 0, PIECE)
             if a == 2:
                 spread_bias()
             if a + 3 < PIECES:
-                load(a + 3, (K, K + K // 2) if a + 3 == PIECES - 1 else ())
+                load(a + 3, (K, K + K // 2) if a + 3 == PIECES - 1 else (K,) if a + 3 >= 4 else ())
 
         xc = const.tile([P, G * M], U32, name="xc", align_bytes=64)
         xs = const.tile([P, G * M], U8, name="xs", align_bytes=64)
@@ -224,9 +224,8 @@ def tile_masklockedlinear_kernel(tc, x, weight, mask, bias, out):
         diag(a, 0)
         squares(a, 0)
         absolute(a - 1)
+        transpose_row(wts[a][:], sg[a][:], 0, 0, SS)
         sums(a - 1, range(32))
-        absolute_cols(0, K)
-        sums_cols(0, K)
         load_x(3)
         for c in range(2):
             lo = K + c * K // 2
@@ -234,6 +233,9 @@ def tile_masklockedlinear_kernel(tc, x, weight, mask, bias, out):
             diag(a, 1, range(8 * c, 8 * c + 8))
             absolute_cols(lo, lo + K // 2)
             sums_cols(lo, lo + K // 2)
+            if c == 1:
+                absolute_row(a, 0)
+                sums(a, row_blocks[0])
             if c == 0:
                 xgs[0] = stream.tile([P, PIECE], BF16, name="xg", tag="m", align_bytes=64)
 
@@ -288,7 +290,7 @@ def tile_masklockedlinear_kernel(tc, x, weight, mask, bias, out):
                 start=(g == 0), stop=(g == G - 1),
             )
 
-        sign_queue = [(s, c) for s in SCALAR_SIGNS for c in range(8)]
+        sign_queue = [(s, c) for s in (6, ) for c in range(8)]
 
         def sign_some(count):
             for c in range(min(count, len(sign_queue))):
@@ -372,6 +374,7 @@ def tile_masklockedlinear_kernel(tc, x, weight, mask, bias, out):
                 )
 
         Q = PIECE // G
+        transpose_row(wts[a][:], sg[a][:], 1, 2, SS)
         transpose_row(xts[0][:], xgs[0][:], 0, 0, SS)
         transpose_row(xts[0][:], xgs[0][:], 1, 2, SS)
         transpose_x(1)
@@ -393,7 +396,7 @@ def tile_masklockedlinear_kernel(tc, x, weight, mask, bias, out):
         transpose_x(3)
         quantise_x(2, range(G))
         quantise_w(0, 3 * Q, 4 * Q)
-        sign_some(2)
+        sign_some(0)
         multiply_t(0, 0)
         sign_some(2)
         tern_abs(1, 0, PIECE)
@@ -403,16 +406,14 @@ def tile_masklockedlinear_kernel(tc, x, weight, mask, bias, out):
         quantise_w(1, 0, PIECE)
         tern_abs(2, 0, PIECE)
         multiply_t(0, 1)
-        transpose_row(wts[a][:], sg[a][:], 0, 0, SS)
-        transpose_row(wts[a][:], sg[a][:], 1, 2, SS)
         multiply_t(1, 0)
         multiply_t(1, 1)
         finish_t(0)
         for i in range(2, PIECES):
-            if i == 5:
-                signs(6, 0, PIECE)
+            if i + 1 in (4, ):
+                signs(i + 1, 0, PIECE)
             if i == 6:
-                absolute(a)
+                absolute_row(a, 1)
                 signs(a, 0, PIECE)
             tern_sign(i, 0, PIECE)
             if i + 1 < PIECES:

@@ -22,9 +22,9 @@ PIECES = N // ROWS
 X_LOADS = M // ROWS
 PIECE = G * ROWS * 4
 COUNT = N * K
-DIAG_BLOCKS = 10
-ONES_N = 14
-T_PIECES = 4
+DIAG_BLOCKS = 11
+ONES_N = 8
+T_PIECES = 5
 SCALAR_SIGNS = (6, )
 
 
@@ -98,11 +98,15 @@ def tile_masklockedlinear_kernel(tc, x, weight, mask, bias, out):
             sl = slice(lo, hi)
             nc.vector.tensor_tensor(out=wts[a][:, sl], in0=wts[a][:, sl], in1=mks[a][:, sl], op=ALU.mult)
 
+        TURN = (0, 1, 2, 3, 7)
+        turn = []
+
         def transpose_row(src, dst, r, first, copies):
             words = src.bitcast(F32)
             dwords = dst.bitcast(F32).rearrange("p (g r j u) -> p g r j u", g=G, r=2, u=2)
             for h in range(2):
-                pt = bank((first + h) % 4, [P, 512])
+                turn.append(h)
+                pt = bank(TURN[len(turn) % len(TURN)], [P, 512])
                 for gg in range(2):
                     for u in range(2):
                         col = r * 1024 + 256 * (2 * h + gg) + 128 * u
@@ -172,16 +176,21 @@ def tile_masklockedlinear_kernel(tc, x, weight, mask, bias, out):
                 absolute(a - 1)
             for r in range(2):
                 transpose_row(wts[a][:], sg[a][:], r, 2 * r, SS)
-                diag(a, r)
+                if r == 0:
+                    diag(a, 0)
                 squares(a, r)
             if a >= 1:
-                sums(a - 1, range(32))
+                sums(a - 1, range(16))
+            diag(a, 1, range(DIAG_BLOCKS // 2))
+            if a >= 1:
+                sums(a - 1, range(16, 32))
+            diag(a, 1, range(DIAG_BLOCKS // 2, DIAG_BLOCKS))
             if 1 <= a < 5:
                 signs(a - 1, 0, PIECE)
             if a == 2:
                 spread_bias()
             if a + 3 < PIECES:
-                load(a + 3, (K, K + K // 2) if a + 3 == PIECES - 1 else (K,) if a + 3 >= 4 else ())
+                load(a + 3, (K, K + K // 2) if a + 3 == PIECES - 1 else (K,) if a + 3 >= 6 else ())
 
         xc = const.tile([P, G * M], U32, name="xc", align_bytes=64)
         xs = const.tile([P, G * M], U8, name="xs", align_bytes=64)
@@ -308,7 +317,7 @@ def tile_masklockedlinear_kernel(tc, x, weight, mask, bias, out):
             if mh == 0:
                 o_t[i] = stream.tile([P, 2 * M], F32, name="o_t", tag="m", align_bytes=64)
             pair = [bank(base + mh * 2 + nt, [P, 512]) for nt in range(2)]
-            if i == 0:
+            if i == 0 or (i == 1 and mh == 0):
                 for g in range(G):
                     for nt in range(2):
                         pass_t(i, pair[nt], mh, nt, g)
@@ -322,11 +331,15 @@ def tile_masklockedlinear_kernel(tc, x, weight, mask, bias, out):
                     if i < T_PIECES - 1 and (mh, nt) != (1, 1):
                         sign_some(1)
 
-        def finish_t(i):
+        ots = {}
+
+        def finish_t(i, half):
             base = ((i + 1) % 2) * 4
-            ot = stream.tile([P, 8 * ROWS], F32, name="ot", tag="w", bufs=4)
+            if half == 0:
+                ots[i] = stream.tile([P, 8 * ROWS], F32, name="ot", tag="w", bufs=4)
+            ot = ots[i]
             cols = slice(i * ROWS, (i + 1) * ROWS)
-            for q in range(4):
+            for q in (2 * half, 2 * half + 1):
                 bt = bank(base + q, [P, 2 * ROWS])
                 for h in range(2):
                     for nt in range(2):
@@ -342,9 +355,10 @@ def tile_masklockedlinear_kernel(tc, x, weight, mask, bias, out):
                         in_=ot[:, (q - 1) * 2 * ROWS:(q + 1) * 2 * ROWS].rearrange("p (i n) -> p i n", i=4),
                     )
 
-        def multiply_n(i):
-            accs[i] = []
-            for q in range(4):
+        def multiply_n(i, half):
+            if half == 0:
+                accs[i] = []
+            for q in (2 * half, 2 * half + 1):
                 acc = bank(((i + 1) % 2) * 4 + q, [P, 2 * ROWS])
                 for h in range(2):
                     for g in range(G):
@@ -401,14 +415,18 @@ def tile_masklockedlinear_kernel(tc, x, weight, mask, bias, out):
         sign_some(2)
         tern_abs(1, 0, PIECE)
         quantise_x(3, range(G))
-        tern_sign(1, 0, PIECE)
         codes(1)
-        quantise_w(1, 0, PIECE)
+        tern_sign(1, 0, Q)
+        for g in range(1, G):
+            tern_sign(1, g * Q, (g + 1) * Q)
+            quantise_w(1, (g - 1) * Q, g * Q)
+        quantise_w(1, 3 * Q, PIECE)
         tern_abs(2, 0, PIECE)
         multiply_t(0, 1)
         multiply_t(1, 0)
+        finish_t(0, 0)
         multiply_t(1, 1)
-        finish_t(0)
+        finish_t(0, 1)
         for i in range(2, PIECES):
             if i + 1 in (4, ):
                 signs(i + 1, 0, PIECE)
@@ -417,18 +435,20 @@ def tile_masklockedlinear_kernel(tc, x, weight, mask, bias, out):
                 signs(a, 0, PIECE)
             tern_sign(i, 0, PIECE)
             if i + 1 < PIECES:
-                tern_abs(i + 1, 0, PIECE)
+                tern_abs(i + 1, 0, PIECE // 2)
             codes(i)
             quantise_w(i, 0, PIECE)
+            if i + 1 < PIECES:
+                tern_abs(i + 1, PIECE // 2, PIECE)
             if i - 2 >= T_PIECES:
                 finish_n(i - 2)
-            if i < T_PIECES:
-                multiply_t(i, 0)
-                multiply_t(i, 1)
-            else:
-                multiply_n(i)
-            if i - 1 < T_PIECES:
-                finish_t(i - 1)
+            for half in range(2):
+                if i < T_PIECES:
+                    multiply_t(i, half)
+                else:
+                    multiply_n(i, half)
+                if i - 1 < T_PIECES:
+                    finish_t(i - 1, half)
             if i == T_PIECES - 1:
                 sign_some(len(sign_queue))
         finish_n(PIECES - 2)

@@ -56,8 +56,8 @@ def tile_masklockedlinear_kernel(tc, x, weight, mask, bias, out):
                 nc.sync.dma_start(out=wts[a][:, part], in_=w_view[a][:, part])
                 nc.sync.dma_start(out=mks[a][:, part], in_=m_view[a][:, part])
 
-        load(0, (K,))
-        load(1, (K,))
+        load(0, ())
+        load(1, ())
 
         ident = const.tile([P, P], F32, name="ident")
         make_identity(nc, ident[:])
@@ -88,7 +88,8 @@ def tile_masklockedlinear_kernel(tc, x, weight, mask, bias, out):
             aw.append(big.tile([P, PIECE], BF16, name="aw%d" % a, tag="aw", align_bytes=64))
             sg.append(big.tile([P, PIECE], BF16, name="sg%d" % a, tag="sg", align_bytes=64))
         n_a = PIECES * 32
-        diag_last = DIAG_BLOCKS * (2 * PIECES - 1) + 16 - 1
+        D_OF = (9,9,10,11,12,12,13,12)
+        diag_last = 2 * sum(D_OF[:7]) + D_OF[7] + 16 - 1
         diag_done = []
 
         def mask_row(a, r):
@@ -98,7 +99,7 @@ def tile_masklockedlinear_kernel(tc, x, weight, mask, bias, out):
             sl = slice(lo, hi)
             nc.vector.tensor_tensor(out=wts[a][:, sl], in0=wts[a][:, sl], in1=mks[a][:, sl], op=ALU.mult)
 
-        TURN = (0, 1, 2, 3, 7)
+        TURN = (0, 1, 2, 3, 7, 6)
         turn = []
 
         def transpose_row(src, dst, r, first, copies):
@@ -119,17 +120,18 @@ def tile_masklockedlinear_kernel(tc, x, weight, mask, bias, out):
         SS = (nc.scalar.copy, nc.scalar.copy)
         SV = (nc.scalar.copy, nc.vector.tensor_copy)
 
-        def diag(a, r, blocks=range(DIAG_BLOCKS)):
-            for b in blocks:
+        def diag(a, r, blocks=None):
+            for b in (range(D_OF[a]) if blocks is None else blocks):
                 i_d = len(diag_done)
                 diag_done.append(b)
                 blk = wts[a][:, r * K + b * P:r * K + (b + 1) * P]
                 nc.tensor.matmul(acc_d[:], lhsT=blk, rhs=blk, start=(i_d == 0), stop=(i_d == diag_last))
 
         def squares(a, r):
-            junk = stream.tile([P, K - DIAG_BLOCKS * P], BF16, name="junk", tag="junk", bufs=2)
+            width = K - D_OF[a] * P
+            junk = stream.tile([P, K - min(D_OF) * P], BF16, name="junk", tag="junk", bufs=2)
             nc.scalar.activation(
-                out=junk[:], in_=wts[a][:, r * K + DIAG_BLOCKS * P:(r + 1) * K], func=ACT.Square,
+                out=junk[:, 0:width], in_=wts[a][:, r * K + D_OF[a] * P:(r + 1) * K], func=ACT.Square,
                 accum_out=zt[:, 2 + 2 * a + r:3 + 2 * a + r],
             )
 
@@ -181,10 +183,10 @@ def tile_masklockedlinear_kernel(tc, x, weight, mask, bias, out):
                 squares(a, r)
             if a >= 1:
                 sums(a - 1, range(16))
-            diag(a, 1, range(DIAG_BLOCKS // 2))
+            diag(a, 1, range(D_OF[a] // 2))
             if a >= 1:
                 sums(a - 1, range(16, 32))
-            diag(a, 1, range(DIAG_BLOCKS // 2, DIAG_BLOCKS))
+            diag(a, 1, range(D_OF[a] // 2, D_OF[a]))
             if 1 <= a < 5:
                 signs(a - 1, 0, PIECE)
             if a == 2:
@@ -255,6 +257,7 @@ def tile_masklockedlinear_kernel(tc, x, weight, mask, bias, out):
         dj = const.tile([P, P], F32, name="dj")
         nc.vector.scalar_tensor_tensor(out=dj[:], in0=acc_d[:], scalar=1.0, in1=ident[:], op0=ALU.mult, op1=ALU.mult, accum_out=zt[:, 1:2])
         nc.vector.tensor_copy(out=zt[:, 0:1], in_=acc_a[:, 0:1])
+        transpose_row(wts[a][:], sg[a][:], 1, 2, SS)
         tot = bank(6, [P, 1 + 2 * PIECES])
         nc.tensor.matmul(tot[:], lhsT=mean_w[:], rhs=zt[:], start=True, stop=True)
         signs(a - 2, 2 * EIGHTH, 4 * EIGHTH)
@@ -388,7 +391,6 @@ def tile_masklockedlinear_kernel(tc, x, weight, mask, bias, out):
                 )
 
         Q = PIECE // G
-        transpose_row(wts[a][:], sg[a][:], 1, 2, SS)
         transpose_row(xts[0][:], xgs[0][:], 0, 0, SS)
         transpose_row(xts[0][:], xgs[0][:], 1, 2, SS)
         transpose_x(1)

@@ -24,8 +24,9 @@ PIECE = G * ROWS * 4
 COUNT = N * K
 DIAG_BLOCKS = 11
 ONES_N = 8
-T_PIECES = 5
-SCALAR_SIGNS = (6, )
+T_HALVES = 9
+N_FIRST = T_HALVES // 2
+SCALAR_SIGNS = (6, 7, )
 
 
 def tile_masklockedlinear_kernel(tc, x, weight, mask, bias, out):
@@ -61,7 +62,7 @@ def tile_masklockedlinear_kernel(tc, x, weight, mask, bias, out):
 
         ident = const.tile([P, P], F32, name="ident")
         make_identity(nc, ident[:])
-        brow = const.tile([P, (PIECES - T_PIECES) * ROWS], BF16, name="brow")
+        brow = const.tile([P, (PIECES - N_FIRST) * ROWS], BF16, name="brow")
         nc.gpsimd.memset(brow[:], 0.0)
         mean_w = const.tile([P, P], F32, name="mean_w")
         nc.vector.memset(mean_w[:], 1.0 / COUNT)
@@ -71,12 +72,12 @@ def tile_masklockedlinear_kernel(tc, x, weight, mask, bias, out):
         nc.vector.memset(bsq_b[:], 0.0)
         bsq = const.tile([P, ROWS], F32, name="bsq")
         bias_t = const.tile([P, 2 * P], F32, name="bias_t")
-        bias_bc = const.tile([P, (PIECES - T_PIECES) * ROWS], BF16, name="bias_bc")
+        bias_bc = const.tile([P, (PIECES - N_FIRST) * ROWS], BF16, name="bias_bc")
         warm = const.tile([P, 1], F32, name="warm")
         nc.scalar.activation(out=warm[:], in_=mean_w[:, 0:1], func=ACT.Sqrt)
 
         nc.sync.dma_start(out=bsq_b[0:PIECES, :], in_=bias.rearrange("(i n) -> i n", n=ROWS))
-        nc.sync.dma_start(out=brow[0:1, :], in_=bias[T_PIECES * ROWS:N].rearrange("(o n) -> o n", o=1))
+        nc.sync.dma_start(out=brow[0:1, :], in_=bias[N_FIRST * ROWS:N].rearrange("(o n) -> o n", o=1))
         load(2, ())
 
         acc_a = bank(4, [P, ONES_N])
@@ -88,7 +89,7 @@ def tile_masklockedlinear_kernel(tc, x, weight, mask, bias, out):
             aw.append(big.tile([P, PIECE], BF16, name="aw%d" % a, tag="aw", align_bytes=64))
             sg.append(big.tile([P, PIECE], BF16, name="sg%d" % a, tag="sg", align_bytes=64))
         n_a = PIECES * 32
-        D_OF = (9,9,10,11,12,12,13,12)
+        D_OF = (10,10,11,11,11,11,12,12)
         diag_last = 2 * sum(D_OF[:7]) + D_OF[7] + 16 - 1
         diag_done = []
 
@@ -164,7 +165,7 @@ def tile_masklockedlinear_kernel(tc, x, weight, mask, bias, out):
             for r in range(2):
                 nc.tensor.transpose(pq[:, r * P:(r + 1) * P], bsq[:].rearrange("p (j r) -> p r j", r=2)[:, r, :], ident[:])
             nc.scalar.copy(out=bias_t[:], in_=pq[:])
-            width = (PIECES - T_PIECES) * ROWS
+            width = (PIECES - N_FIRST) * ROWS
             for c in range(0, width, 512):
                 w = min(512, width - c)
                 pb = bank(6 + (c // 512 + 1) % 2, [P, w])
@@ -172,6 +173,8 @@ def tile_masklockedlinear_kernel(tc, x, weight, mask, bias, out):
                 nc.scalar.copy(out=bias_bc[:, c:c + w], in_=pb[:])
 
         for a in range(PIECES - 1):
+            if a == 6:
+                signs(4, 0, PIECE // 2)
             mask_row(a, 0)
             mask_row(a, 1)
             if a >= 1:
@@ -234,6 +237,7 @@ def tile_masklockedlinear_kernel(tc, x, weight, mask, bias, out):
         mask_row(a, 0)
         diag(a, 0)
         squares(a, 0)
+        signs(4, HALF, PIECE)
         absolute(a - 1)
         transpose_row(wts[a][:], sg[a][:], 0, 0, SS)
         sums(a - 1, range(32))
@@ -271,6 +275,9 @@ def tile_masklockedlinear_kernel(tc, x, weight, mask, bias, out):
         nc.vector.tensor_scalar(out=st[:, 4:5], in0=st[:, 1:2], scalar1=2.0, scalar2=2e-8, op0=ALU.mult, op1=ALU.add)
         nc.vector.tensor_scalar(out=st[:, 5:6], in0=st[:, 1:2], scalar1=1.0, scalar2=1e-8, op0=ALU.mult, op1=ALU.add)
 
+        def is_t(i, half):
+            return 2 * i + half < T_HALVES
+
         wc = {}
         ws = {}
         accs = {}
@@ -302,7 +309,7 @@ def tile_masklockedlinear_kernel(tc, x, weight, mask, bias, out):
                 start=(g == 0), stop=(g == G - 1),
             )
 
-        sign_queue = [(s, c) for s in (6, ) for c in range(8)]
+        sign_queue = [(s, c) for s in (6, 7, ) for c in range(8)]
 
         def sign_some(count):
             for c in range(min(count, len(sign_queue))):
@@ -331,7 +338,7 @@ def tile_masklockedlinear_kernel(tc, x, weight, mask, bias, out):
                     for g in range(G):
                         pass_t(i, pair[nt], mh, nt, g)
                     out_t(i, pair[nt], mh, nt)
-                    if i < T_PIECES - 1 and (mh, nt) != (1, 1):
+                    if i < N_FIRST and (mh, nt) != (1, 1):
                         sign_some(1)
 
         ots = {}
@@ -359,8 +366,7 @@ def tile_masklockedlinear_kernel(tc, x, weight, mask, bias, out):
                     )
 
         def multiply_n(i, half):
-            if half == 0:
-                accs[i] = []
+            accs.setdefault(i, {})
             for q in (2 * half, 2 * half + 1):
                 acc = bank(((i + 1) % 2) * 4 + q, [P, 2 * ROWS])
                 for h in range(2):
@@ -372,13 +378,15 @@ def tile_masklockedlinear_kernel(tc, x, weight, mask, bias, out):
                             rhs=wc[i][:, g * ROWS:(g + 1) * ROWS].bitcast(FP8X4), rhs_scale=ws[i][:, g * ROWS:(g + 1) * ROWS],
                             start=(g == 0), stop=(g == G - 1),
                         )
-                accs[i].append(acc)
+                accs[i][q] = acc
 
-        def finish_n(i):
-            ot = stream.tile([P, 8 * ROWS], F32, name="ot", tag="w", bufs=4)
+        def finish_n(i, half):
+            if half == 0:
+                ots[i] = stream.tile([P, 8 * ROWS], F32, name="ot", tag="w", bufs=4)
+            ot = ots[i]
             cols = slice(i * ROWS, (i + 1) * ROWS)
-            bcols = slice((i - T_PIECES) * ROWS, (i - T_PIECES + 1) * ROWS)
-            for q in range(4):
+            bcols = slice((i - N_FIRST) * ROWS, (i - N_FIRST + 1) * ROWS)
+            for q in (2 * half, 2 * half + 1):
                 nc.vector.tensor_tensor(
                     out=ot[:, q * 2 * ROWS:(q + 1) * 2 * ROWS].rearrange("p (h j r) -> p h j r", h=2, r=2),
                     in0=accs[i][q][:].rearrange("p (h r j) -> p h j r", h=2, r=2),
@@ -395,26 +403,19 @@ def tile_masklockedlinear_kernel(tc, x, weight, mask, bias, out):
         transpose_row(xts[0][:], xgs[0][:], 1, 2, SS)
         transpose_x(1)
         codes(0)
-        tern_abs(0, 0, Q)
-        tern_abs(0, Q, 2 * Q)
-        tern_sign(0, 0, Q)
-        tern_abs(0, 2 * Q, 3 * Q)
-        tern_sign(0, Q, 2 * Q)
-        quantise_w(0, 0, Q)
+        tern_abs(0, 0, PIECE // 2)
+        tern_abs(0, PIECE // 2, PIECE)
+        tern_sign(0, 0, PIECE // 2)
+        tern_sign(0, PIECE // 2, PIECE)
         quantise_x(0, range(G))
-        tern_abs(0, 3 * Q, 4 * Q)
-        tern_sign(0, 2 * Q, 3 * Q)
-        quantise_w(0, Q, 2 * Q)
-        quantise_x(1, range(G))
-        tern_sign(0, 3 * Q, 4 * Q)
-        quantise_w(0, 2 * Q, 3 * Q)
+        quantise_w(0, 0, PIECE)
         transpose_x(2)
         transpose_x(3)
-        quantise_x(2, range(G))
-        quantise_w(0, 3 * Q, 4 * Q)
+        quantise_x(1, range(G))
         sign_some(0)
         multiply_t(0, 0)
         sign_some(2)
+        quantise_x(2, range(G))
         tern_abs(1, 0, PIECE)
         quantise_x(3, range(G))
         codes(1)
@@ -425,33 +426,33 @@ def tile_masklockedlinear_kernel(tc, x, weight, mask, bias, out):
         quantise_w(1, 3 * Q, PIECE)
         tern_abs(2, 0, PIECE)
         multiply_t(0, 1)
+        sign_some(3)
         multiply_t(1, 0)
         finish_t(0, 0)
         multiply_t(1, 1)
         finish_t(0, 1)
         for i in range(2, PIECES):
-            if i + 1 in (4, ):
-                signs(i + 1, 0, PIECE)
-            if i == 6:
+            if i == 2:
                 absolute_row(a, 1)
-                signs(a, 0, PIECE)
             tern_sign(i, 0, PIECE)
             if i + 1 < PIECES:
-                tern_abs(i + 1, 0, PIECE // 2)
+                tern_abs(i + 1, 0, PIECE // 4)
             codes(i)
             quantise_w(i, 0, PIECE)
             if i + 1 < PIECES:
-                tern_abs(i + 1, PIECE // 2, PIECE)
-            if i - 2 >= T_PIECES:
-                finish_n(i - 2)
+                tern_abs(i + 1, PIECE // 4, PIECE)
             for half in range(2):
-                if i < T_PIECES:
+                if not is_t(i - 2, half):
+                    finish_n(i - 2, half)
+            for half in range(2):
+                if is_t(i, half):
                     multiply_t(i, half)
                 else:
                     multiply_n(i, half)
-                if i - 1 < T_PIECES:
+                if is_t(i - 1, half):
                     finish_t(i - 1, half)
-            if i == T_PIECES - 1:
+            if i == N_FIRST:
                 sign_some(len(sign_queue))
-        finish_n(PIECES - 2)
-        finish_n(PIECES - 1)
+        for i in (PIECES - 2, PIECES - 1):
+            for half in range(2):
+                finish_n(i, half)

@@ -24,7 +24,7 @@ PIECE = G * ROWS * 4
 COUNT = N * K
 DIAG_BLOCKS = 11
 ONES_N = 8
-T_HALVES = 9
+T_HALVES = 8
 N_FIRST = T_HALVES // 2
 SCALAR_SIGNS = (6, 7, )
 
@@ -55,7 +55,7 @@ def tile_masklockedlinear_kernel(tc, x, weight, mask, bias, out):
             for lo, hi in zip((0,) + cuts, cuts + (2 * K,)):
                 part = slice(lo, hi)
                 nc.sync.dma_start(out=wts[a][:, part], in_=w_view[a][:, part])
-                nc.sync.dma_start(out=mks[a][:, part], in_=m_view[a][:, part])
+                nc.scalar.dma_start(out=mks[a][:, part], in_=m_view[a][:, part])
 
         load(0, ())
         load(1, ())
@@ -100,7 +100,7 @@ def tile_masklockedlinear_kernel(tc, x, weight, mask, bias, out):
             sl = slice(lo, hi)
             nc.vector.tensor_tensor(out=wts[a][:, sl], in0=wts[a][:, sl], in1=mks[a][:, sl], op=ALU.mult)
 
-        TURN = (0, 1, 2, 3, 7, 6)
+        TURN = (0, 1, 2, 3, 7)
         turn = []
 
         def transpose_row(src, dst, r, first, copies):
@@ -195,7 +195,7 @@ def tile_masklockedlinear_kernel(tc, x, weight, mask, bias, out):
             if a == 2:
                 spread_bias()
             if a + 3 < PIECES:
-                load(a + 3, (K, K + K // 2) if a + 3 == PIECES - 1 else (K,) if a + 3 >= 6 else ())
+                load(a + 3, (K,) if a + 3 == PIECES - 1 else (K,) if a + 3 >= 6 else ())
 
         xc = const.tile([P, G * M], U32, name="xc", align_bytes=64)
         xs = const.tile([P, G * M], U8, name="xs", align_bytes=64)
@@ -204,7 +204,8 @@ def tile_masklockedlinear_kernel(tc, x, weight, mask, bias, out):
 
         def load_x(b):
             xts[b] = stream.tile([P, 2 * K], BF16, name="xt", tag="w", bufs=4)
-            nc.sync.dma_start(out=xts[b][:].rearrange("p (r k) -> p r k", r=2), in_=x_view[b])
+            queue = nc.scalar if b < X_LOADS - 1 else nc.sync
+            queue.dma_start(out=xts[b][:].rearrange("p (r k) -> p r k", r=2), in_=x_view[b])
 
         def transpose_x(b):
             xgs[b] = stream.tile([P, PIECE], BF16, name="xg", tag="m", align_bytes=64)
@@ -242,20 +243,23 @@ def tile_masklockedlinear_kernel(tc, x, weight, mask, bias, out):
         transpose_row(wts[a][:], sg[a][:], 0, 0, SS)
         sums(a - 1, range(32))
         load_x(3)
-        for c in range(2):
-            lo = K + c * K // 2
-            mask_cols(a, lo, lo + K // 2)
-            diag(a, 1, range(8 * c, 8 * c + 8))
-            absolute_cols(lo, lo + K // 2)
-            sums_cols(lo, lo + K // 2)
-            if c == 1:
-                absolute_row(a, 0)
-                sums(a, row_blocks[0])
-            if c == 0:
-                xgs[0] = stream.tile([P, PIECE], BF16, name="xg", tag="m", align_bytes=64)
-
+        mask_row(a, 1)
+        diag(a, 1, range(16))
+        absolute_row(a, 0)
+        sums(a, row_blocks[0])
+        absolute_cols(K, 2 * K)
+        sums_cols(K, 2 * K)
+        xgs[0] = stream.tile([P, PIECE], BF16, name="xg", tag="m", align_bytes=64)
         EIGHTH = PIECE // 8
-        signs(a - 2, 0, 2 * EIGHTH)
+        fillers = [(p, e) for p in (5,) for e in range(8)]
+        fillers.reverse()
+
+        def fill(count):
+            for n in range(count):
+                p, e = fillers.pop()
+                signs(p, e * EIGHTH, (e + 1) * EIGHTH)
+
+        fill(2)
         st = const.tile([P, 8], F32, name="st")
         thr = const.tile([P, 1], F32, name="thr")
         dj = const.tile([P, P], F32, name="dj")
@@ -264,16 +268,16 @@ def tile_masklockedlinear_kernel(tc, x, weight, mask, bias, out):
         transpose_row(wts[a][:], sg[a][:], 1, 2, SS)
         tot = bank(6, [P, 1 + 2 * PIECES])
         nc.tensor.matmul(tot[:], lhsT=mean_w[:], rhs=zt[:], start=True, stop=True)
-        signs(a - 2, 2 * EIGHTH, 4 * EIGHTH)
+        fill(2)
         nc.vector.tensor_reduce(out=st[:, 0:1], in_=tot[:, 1:], axis=mybir.AxisListType.X, op=ALU.add)
-        nc.vector.tensor_copy(out=st[:, 1:2], in_=tot[:, 0:1])
-        signs(a - 2, 4 * EIGHTH, 5 * EIGHTH)
-        nc.vector.scalar_tensor_tensor(out=st[:, 2:3], in0=st[:, 1:2], scalar=st[:, 1:2], in1=st[:, 0:1], op0=ALU.mult, op1=ALU.subtract)
+        nc.vector.tensor_scalar(out=st[:, 4:5], in0=tot[:, 0:1], scalar1=2.0, scalar2=2e-8, op0=ALU.mult, op1=ALU.add)
+        nc.vector.tensor_scalar(out=st[:, 5:6], in0=tot[:, 0:1], scalar1=1.0, scalar2=1e-8, op0=ALU.mult, op1=ALU.add)
+        fill(1)
+        nc.vector.scalar_tensor_tensor(out=st[:, 2:3], in0=tot[:, 0:1], scalar=tot[:, 0:1], in1=st[:, 0:1], op0=ALU.mult, op1=ALU.subtract)
+        fill(2)
         nc.vector.tensor_scalar(out=st[:, 3:4], in0=st[:, 2:3], scalar1=-0.25 * COUNT / (COUNT - 1), scalar2=0.0, op0=ALU.mult, op1=ALU.max)
         nc.scalar.activation(out=thr[:], in_=st[:, 3:4], func=ACT.Sqrt)
-        signs(a - 2, 5 * EIGHTH, PIECE)
-        nc.vector.tensor_scalar(out=st[:, 4:5], in0=st[:, 1:2], scalar1=2.0, scalar2=2e-8, op0=ALU.mult, op1=ALU.add)
-        nc.vector.tensor_scalar(out=st[:, 5:6], in0=st[:, 1:2], scalar1=1.0, scalar2=1e-8, op0=ALU.mult, op1=ALU.add)
+        fill(1)
 
         def is_t(i, half):
             return 2 * i + half < T_HALVES
@@ -327,7 +331,7 @@ def tile_masklockedlinear_kernel(tc, x, weight, mask, bias, out):
             if mh == 0:
                 o_t[i] = stream.tile([P, 2 * M], F32, name="o_t", tag="m", align_bytes=64)
             pair = [bank(base + mh * 2 + nt, [P, 512]) for nt in range(2)]
-            if i == 0 or (i == 1 and mh == 0):
+            if i == 0:
                 for g in range(G):
                     for nt in range(2):
                         pass_t(i, pair[nt], mh, nt, g)
@@ -424,7 +428,8 @@ def tile_masklockedlinear_kernel(tc, x, weight, mask, bias, out):
             tern_sign(1, g * Q, (g + 1) * Q)
             quantise_w(1, (g - 1) * Q, g * Q)
         quantise_w(1, 3 * Q, PIECE)
-        tern_abs(2, 0, PIECE)
+        tern_abs(2, 0, HALF)
+        tern_abs(2, HALF, PIECE)
         multiply_t(0, 1)
         sign_some(3)
         multiply_t(1, 0)
@@ -434,13 +439,16 @@ def tile_masklockedlinear_kernel(tc, x, weight, mask, bias, out):
         for i in range(2, PIECES):
             if i == 2:
                 absolute_row(a, 1)
-            tern_sign(i, 0, PIECE)
-            if i + 1 < PIECES:
-                tern_abs(i + 1, 0, PIECE // 4)
+            tern_sign(i, 0, HALF)
+            tern_sign(i, HALF, PIECE)
             codes(i)
-            quantise_w(i, 0, PIECE)
             if i + 1 < PIECES:
-                tern_abs(i + 1, PIECE // 4, PIECE)
+                tern_abs(i + 1, 0, HALF)
+                quantise_w(i, 0, PIECE)
+                tern_abs(i + 1, HALF, PIECE)
+            else:
+                quantise_w(i, 0, HALF)
+                quantise_w(i, HALF, PIECE)
             for half in range(2):
                 if not is_t(i - 2, half):
                     finish_n(i - 2, half)

@@ -55,7 +55,7 @@ def tile_masklockedlinear_kernel(tc, x, weight, mask, bias, out):
             for lo, hi in zip((0,) + cuts, cuts + (2 * K,)):
                 part = slice(lo, hi)
                 nc.sync.dma_start(out=wts[a][:, part], in_=w_view[a][:, part])
-                nc.scalar.dma_start(out=mks[a][:, part], in_=m_view[a][:, part])
+                nc.sync.dma_start(out=mks[a][:, part], in_=m_view[a][:, part])
 
         load(0, ())
         load(1, ())
@@ -89,7 +89,7 @@ def tile_masklockedlinear_kernel(tc, x, weight, mask, bias, out):
             aw.append(big.tile([P, PIECE], BF16, name="aw%d" % a, tag="aw", align_bytes=64))
             sg.append(big.tile([P, PIECE], BF16, name="sg%d" % a, tag="sg", align_bytes=64))
         n_a = PIECES * 32
-        D_OF = (10,10,11,11,11,11,12,12)
+        D_OF = (10,10,10,10,12,12,12,12)
         diag_last = 2 * sum(D_OF[:7]) + D_OF[7] + 16 - 1
         diag_done = []
 
@@ -204,8 +204,7 @@ def tile_masklockedlinear_kernel(tc, x, weight, mask, bias, out):
 
         def load_x(b):
             xts[b] = stream.tile([P, 2 * K], BF16, name="xt", tag="w", bufs=4)
-            queue = nc.scalar if b < X_LOADS - 1 else nc.sync
-            queue.dma_start(out=xts[b][:].rearrange("p (r k) -> p r k", r=2), in_=x_view[b])
+            nc.sync.dma_start(out=xts[b][:].rearrange("p (r k) -> p r k", r=2), in_=x_view[b])
 
         def transpose_x(b):
             xgs[b] = stream.tile([P, PIECE], BF16, name="xg", tag="m", align_bytes=64)
@@ -331,7 +330,7 @@ def tile_masklockedlinear_kernel(tc, x, weight, mask, bias, out):
             if mh == 0:
                 o_t[i] = stream.tile([P, 2 * M], F32, name="o_t", tag="m", align_bytes=64)
             pair = [bank(base + mh * 2 + nt, [P, 512]) for nt in range(2)]
-            if i == 0:
+            if i == 0 or (i == 1 and mh == 0):
                 for g in range(G):
                     for nt in range(2):
                         pass_t(i, pair[nt], mh, nt, g)
@@ -423,15 +422,14 @@ def tile_masklockedlinear_kernel(tc, x, weight, mask, bias, out):
         tern_abs(1, 0, PIECE)
         quantise_x(3, range(G))
         codes(1)
-        tern_sign(1, 0, Q)
-        for g in range(1, G):
-            tern_sign(1, g * Q, (g + 1) * Q)
-            quantise_w(1, (g - 1) * Q, g * Q)
-        quantise_w(1, 3 * Q, PIECE)
+        tern_sign(1, 0, HALF)
+        tern_sign(1, HALF, PIECE)
+        quantise_w(1, 0, HALF)
+        quantise_w(1, HALF, PIECE)
         tern_abs(2, 0, HALF)
         tern_abs(2, HALF, PIECE)
         multiply_t(0, 1)
-        sign_some(3)
+        sign_some(2)
         multiply_t(1, 0)
         finish_t(0, 0)
         multiply_t(1, 1)

from contextlib import ExitStack

import concourse.mybir as mybir
from concourse.masks import make_identity

FLOPS = 2 * 1024 * 2048 * 2048

F32 = mybir.dt.float32
BF16 = mybir.dt.bfloat16
I32 = mybir.dt.int32
U32 = mybir.dt.uint32
U8 = mybir.dt.uint8
FP8X4 = mybir.dt.float8_e4m3fn_x4
ALU = mybir.AluOpType
ACT = mybir.ActivationFunctionType

P = 128
M, K, N = 1024, 2048, 2048
G = K // 512
ROWS = 256
PIECES = N // ROWS
X_LOADS = M // ROWS
PIECE = G * ROWS * 4
COUNT = N * K
DIAG_BLOCKS = 11
ONES_N = 8
T_HALVES = 8
N_FIRST = T_HALVES // 2
SCALAR_SIGNS = (6, 7, )


def tile_masklockedlinear_kernel(tc, x, weight, mask, bias, out):
    nc = tc.nc
    with ExitStack() as ctx:
        const = ctx.enter_context(tc.tile_pool(name="const", bufs=1))
        stream = ctx.enter_context(tc.tile_pool(name="stream", bufs=3))
        big = ctx.enter_context(tc.tile_pool(name="big", bufs=PIECES))
        psum = ctx.enter_context(tc.psum_pool(name="psum", bufs=1))
        ctx.enter_context(tc.manual_schedule())

        def bank(i, shape):
            return psum.tile(shape, F32, name="bank%d" % i, tag="bank%d" % i)

        w_view = weight.rearrange("(a p r) k -> a p (r k)", p=P, r=2)
        m_view = mask.rearrange("(a p r) k -> a p (r k)", p=P, r=2)
        x_view = x.rearrange("(b r p) k -> b p r k", p=P, r=2)
        o_view = out.rearrange("(i p) n -> p i n", p=P)

        wts = {}
        mks = {}

        def load(a, cuts):
            wts[a] = stream.tile([P, 2 * K], BF16, name="wt", tag="w", bufs=4)
            mks[a] = stream.tile([P, 2 * K], BF16, name="mk", tag="m", align_bytes=64)
            for lo, hi in zip((0,) + cuts, cuts + (2 * K,)):
                part = slice(lo, hi)
                nc.sync.dma_start(out=wts[a][:, part], in_=w_view[a][:, part])
                nc.sync.dma_start(out=mks[a][:, part], in_=m_view[a][:, part])

        load(0, ())
        load(1, ())

        ident = const.tile([P, P], F32, name="ident")
        make_identity(nc, ident[:])
        brow = const.tile([P, (PIECES - N_FIRST) * ROWS], BF16, name="brow")
        nc.gpsimd.memset(brow[:], 0.0)
        mean_w = const.tile([P, P], F32, name="mean_w")
        nc.vector.memset(mean_w[:], 1.0 / COUNT)
        ones_b = const.tile([P, P], BF16, name="ones_b")
        nc.vector.memset(ones_b[:], 1.0)
        bsq_b = const.tile([P, ROWS], BF16, name="bsq_b")
        nc.vector.memset(bsq_b[:], 0.0)
        bsq = const.tile([P, ROWS], F32, name="bsq")
        bias_t = const.tile([P, 2 * P], F32, name="bias_t")
        bias_bc = const.tile([P, (PIECES - N_FIRST) * ROWS], BF16, name="bias_bc")
        warm = const.tile([P, 1], F32, name="warm")
        nc.scalar.activation(out=warm[:], in_=mean_w[:, 0:1], func=ACT.Sqrt)

        nc.sync.dma_start(out=bsq_b[0:PIECES, :], in_=bias.rearrange("(i n) -> i n", n=ROWS))
        nc.sync.dma_start(out=brow[0:1, :], in_=bias[N_FIRST * ROWS:N].rearrange("(o n) -> o n", o=1))
        load(2, ())

        acc_a = bank(4, [P, ONES_N])
        acc_d = bank(5, [P, P])
        zt = const.tile([P, 1 + 2 * PIECES], F32, name="zt")
        aw = []
        sg = []
        for a in range(PIECES):
            aw.append(big.tile([P, PIECE], BF16, name="aw%d" % a, tag="aw", align_bytes=64))
            sg.append(big.tile([P, PIECE], BF16, name="sg%d" % a, tag="sg", align_bytes=64))
        n_a = PIECES * 32
        D_OF = (10,10,10,10,12,12,12,12)
        diag_last = 2 * sum(D_OF[:7]) + D_OF[7] + 16 - 1
        diag_done = []

        def mask_row(a, r):
            mask_cols(a, r * K, (r + 1) * K)

        def mask_cols(a, lo, hi):
            sl = slice(lo, hi)
            nc.vector.tensor_tensor(out=wts[a][:, sl], in0=wts[a][:, sl], in1=mks[a][:, sl], op=ALU.mult)

        TURN = (0, 1, 2, 3, 7)
        turn = []

        def transpose_row(src, dst, r, first, copies):
            words = src.bitcast(F32)
            dwords = dst.bitcast(F32).rearrange("p (g r j u) -> p g r j u", g=G, r=2, u=2)
            for h in range(2):
                turn.append(h)
                pt = bank(TURN[len(turn) % len(TURN)], [P, 512])
                for gg in range(2):
                    for u in range(2):
                        col = r * 1024 + 256 * (2 * h + gg) + 128 * u
                        nc.tensor.transpose(pt[:, (2 * gg + u) * P:(2 * gg + u + 1) * P], words[:, col:col + P], ident[:])
                copies[h](
                    out=dwords[:, 2 * h:2 * h + 2, r, :, :],
                    in_=pt[:].rearrange("p (g u j) -> p g j u", g=2, u=2),
                )

        SS = (nc.scalar.copy, nc.scalar.copy)
        SV = (nc.scalar.copy, nc.vector.tensor_copy)

        def diag(a, r, blocks=None):
            for b in (range(D_OF[a]) if blocks is None else blocks):
                i_d = len(diag_done)
                diag_done.append(b)
                blk = wts[a][:, r * K + b * P:r * K + (b + 1) * P]
                nc.tensor.matmul(acc_d[:], lhsT=blk, rhs=blk, start=(i_d == 0), stop=(i_d == diag_last))

        def squares(a, r):
            width = K - D_OF[a] * P
            junk = stream.tile([P, K - min(D_OF) * P], BF16, name="junk", tag="junk", bufs=2)
            nc.scalar.activation(
                out=junk[:, 0:width], in_=wts[a][:, r * K + D_OF[a] * P:(r + 1) * K], func=ACT.Square,
                accum_out=zt[:, 2 + 2 * a + r:3 + 2 * a + r],
            )

        def absolute(a):
            nc.vector.tensor_single_scalar(out=aw[a][:].bitcast(I32), in_=sg[a][:].bitcast(I32), scalar=0x7FFF7FFF, op=ALU.bitwise_and)

        def absolute_row(a, r):
            src = sg[a][:].bitcast(I32).rearrange("p (g r c) -> p g r c", g=G, r=2)
            dst = aw[a][:].bitcast(I32).rearrange("p (g r c) -> p g r c", g=G, r=2)
            nc.vector.tensor_single_scalar(out=dst[:, :, r, :], in_=src[:, :, r, :], scalar=0x7FFF7FFF, op=ALU.bitwise_and)

        def sums(a, blocks):
            for n, q in enumerate(blocks):
                sums_done.append(q)
                i_a = len(sums_done) - 1
                nc.tensor.matmul(acc_a[:], lhsT=aw[a][:, q * P:(q + 1) * P], rhs=ones_b[:, 0:ONES_N], start=(i_a == 0), stop=(i_a == n_a - 1))

        sums_done = []
        row_blocks = [[q for q in range(32) if (q // 4) % 2 == r] for r in range(2)]

        def signs_s(a, lo, hi):
            nc.scalar.activation(out=sg[a][:, lo:hi], in_=sg[a][:, lo:hi], func=ACT.Sign)

        def signs(a, lo, hi):
            nc.vector.tensor_scalar(out=sg[a][:, lo:hi], in0=sg[a][:, lo:hi], scalar1=0.0, scalar2=0.5, op0=ALU.is_ge, op1=ALU.subtract)

        def spread_bias():
            nc.vector.tensor_copy(out=bsq[:], in_=bsq_b[:])
            pq = bank(6, [P, 2 * P])
            for r in range(2):
                nc.tensor.transpose(pq[:, r * P:(r + 1) * P], bsq[:].rearrange("p (j r) -> p r j", r=2)[:, r, :], ident[:])
            nc.scalar.copy(out=bias_t[:], in_=pq[:])
            width = (PIECES - N_FIRST) * ROWS
            for c in range(0, width, 512):
                w = min(512, width - c)
                pb = bank(6 + (c // 512 + 1) % 2, [P, w])
                nc.tensor.matmul(pb[:], lhsT=ones_b[:], rhs=brow[:, c:c + w], start=True, stop=True)
                nc.scalar.copy(out=bias_bc[:, c:c + w], in_=pb[:])

        for a in range(PIECES - 1):
            if a == 6:
                signs(4, 0, PIECE // 2)
            mask_row(a, 0)
            mask_row(a, 1)
            if a >= 1:
                absolute(a - 1)
            for r in range(2):
                transpose_row(wts[a][:], sg[a][:], r, 2 * r, SS)
                if r == 0:
                    diag(a, 0)
                squares(a, r)
            if a >= 1:
                sums(a - 1, range(16))
            diag(a, 1, range(D_OF[a] // 2))
            if a >= 1:
                sums(a - 1, range(16, 32))
            diag(a, 1, range(D_OF[a] // 2, D_OF[a]))
            if 1 <= a < 5:
                signs(a - 1, 0, PIECE)
            if a == 2:
                spread_bias()
            if a + 3 < PIECES:
                load(a + 3, (K,) if a + 3 == PIECES - 1 else (K,) if a + 3 >= 6 else ())

        xc = const.tile([P, G * M], U32, name="xc", align_bytes=64)
        xs = const.tile([P, G * M], U8, name="xs", align_bytes=64)
        xts = {}
        xgs = {}

        def load_x(b):
            xts[b] = stream.tile([P, 2 * K], BF16, name="xt", tag="w", bufs=4)
            nc.sync.dma_start(out=xts[b][:].rearrange("p (r k) -> p r k", r=2), in_=x_view[b])

        def transpose_x(b):
            xgs[b] = stream.tile([P, PIECE], BF16, name="xg", tag="m", align_bytes=64)
            for r in range(2):
                transpose_row(xts[b][:], xgs[b][:], r, 2 * r, SS)

        def quantise_x(b, passes):
            for g in passes:
                lo = g * M + b * ROWS
                nc.vector.quantize_mx(
                    out=xc[:, lo:lo + ROWS].bitcast(FP8X4), scales=xs[:, lo:lo + ROWS],
                    in_=xgs[b][:, g * 4 * ROWS:(g + 1) * 4 * ROWS],
                )

        load_x(0)
        load_x(1)
        load_x(2)
        a = PIECES - 1
        HALF = PIECE // 2
        absn = const.tile([P, 2 * K], BF16, name="absn")

        def absolute_cols(lo, hi):
            nc.vector.tensor_single_scalar(out=absn[:, lo:hi].bitcast(I32), in_=wts[a][:, lo:hi].bitcast(I32), scalar=0x7FFF7FFF, op=ALU.bitwise_and)

        def sums_cols(lo, hi):
            for q in range(lo // P, hi // P):
                sums_done.append(q)
                nc.tensor.matmul(acc_a[:], lhsT=absn[:, q * P:(q + 1) * P], rhs=ones_b[:, 0:ONES_N], start=False, stop=(len(sums_done) == n_a))

        mask_row(a, 0)
        diag(a, 0)
        squares(a, 0)
        signs(4, HALF, PIECE)
        absolute(a - 1)
        transpose_row(wts[a][:], sg[a][:], 0, 0, SS)
        sums(a - 1, range(32))
        load_x(3)
        mask_row(a, 1)
        diag(a, 1, range(16))
        absolute_row(a, 0)
        sums(a, row_blocks[0])
        absolute_cols(K, 2 * K)
        sums_cols(K, 2 * K)
        xgs[0] = stream.tile([P, PIECE], BF16, name="xg", tag="m", align_bytes=64)
        EIGHTH = PIECE // 8
        fillers = [(p, e) for p in (5,) for e in range(8)]
        fillers.reverse()

        def fill(count):
            for n in range(count):
                p, e = fillers.pop()
                signs(p, e * EIGHTH, (e + 1) * EIGHTH)

        fill(2)
        st = const.tile([P, 8], F32, name="st")
        thr = const.tile([P, 1], F32, name="thr")
        dj = const.tile([P, P], F32, name="dj")
        nc.vector.scalar_tensor_tensor(out=dj[:], in0=acc_d[:], scalar=1.0, in1=ident[:], op0=ALU.mult, op1=ALU.mult, accum_out=zt[:, 1:2])
        nc.vector.tensor_copy(out=zt[:, 0:1], in_=acc_a[:, 0:1])
        transpose_row(wts[a][:], sg[a][:], 1, 2, SS)
        tot = bank(6, [P, 1 + 2 * PIECES])
        nc.tensor.matmul(tot[:], lhsT=mean_w[:], rhs=zt[:], start=True, stop=True)
        fill(2)
        nc.vector.tensor_reduce(out=st[:, 0:1], in_=tot[:, 1:], axis=mybir.AxisListType.X, op=ALU.add)
        nc.vector.tensor_scalar(out=st[:, 4:5], in0=tot[:, 0:1], scalar1=2.0, scalar2=2e-8, op0=ALU.mult, op1=ALU.add)
        nc.vector.tensor_scalar(out=st[:, 5:6], in0=tot[:, 0:1], scalar1=1.0, scalar2=1e-8, op0=ALU.mult, op1=ALU.add)
        fill(1)
        nc.vector.scalar_tensor_tensor(out=st[:, 2:3], in0=tot[:, 0:1], scalar=tot[:, 0:1], in1=st[:, 0:1], op0=ALU.mult, op1=ALU.subtract)
        fill(2)
        nc.vector.tensor_scalar(out=st[:, 3:4], in0=st[:, 2:3], scalar1=-0.25 * COUNT / (COUNT - 1), scalar2=0.0, op0=ALU.mult, op1=ALU.max)
        nc.scalar.activation(out=thr[:], in_=st[:, 3:4], func=ACT.Sqrt)
        fill(1)

        def is_t(i, half):
            return 2 * i + half < T_HALVES

        wc = {}
        ws = {}
        accs = {}
        o_t = {}

        def tern_abs(i, lo, hi):
            nc.vector.tensor_scalar(out=aw[i][:, lo:hi], in0=aw[i][:, lo:hi], scalar1=thr[:, 0:1], scalar2=st[:, 5:6] if i in SCALAR_SIGNS else st[:, 4:5], op0=ALU.is_gt, op1=ALU.mult)

        def tern_sign(i, lo, hi):
            nc.vector.tensor_tensor(out=sg[i][:, lo:hi], in0=aw[i][:, lo:hi], in1=sg[i][:, lo:hi], op=ALU.mult)

        def codes(i):
            if i == 0:
                wc[i] = const.tile([P, G * ROWS], U32, name="wc0", align_bytes=64)
                ws[i] = const.tile([P, G * ROWS], U8, name="ws0", align_bytes=64)
            else:
                wc[i] = big.tile([P, G * ROWS], U32, name="wc%d" % i, tag="aw", align_bytes=64)
                ws[i] = big.tile([P, G * ROWS], U8, name="ws%d" % i, tag="sg", align_bytes=64)

        def quantise_w(i, lo, hi):
            nc.vector.quantize_mx(out=wc[i][:, lo // 4:hi // 4].bitcast(FP8X4), scales=ws[i][:, lo // 4:hi // 4], in_=sg[i][:, lo:hi])

        def pass_t(i, acc, mh, nt, g):
            lo = g * ROWS + nt * P
            xo = g * M + mh * 512
            nc.tensor.matmul_mx(
                out=acc[:], lhsT=wc[i][:, lo:lo + P].bitcast(FP8X4), lhsT_scale=ws[i][:, lo:lo + P],
                rhs=xc[:, xo:xo + 512].bitcast(FP8X4), rhs_scale=xs[:, xo:xo + 512],
                start=(g == 0), stop=(g == G - 1),
            )

        sign_queue = [(s, c) for s in (6, 7, ) for c in range(8)]

        def sign_some(count):
            for c in range(min(count, len(sign_queue))):
                s, c = sign_queue.pop(0)
                signs_s(s, c * EIGHTH, (c + 1) * EIGHTH)

        def out_t(i, acc, mh, nt):
            nc.scalar.activation(
                out=o_t[i][:, nt * M + mh * 512:nt * M + (mh + 1) * 512], in_=acc[:], func=ACT.Identity,
                bias=bias_t[:, nt * P + i:nt * P + i + 1], scale=1.0,
            )

        def multiply_t(i, mh):
            base = ((i + 1) % 2) * 4
            if mh == 0:
                o_t[i] = stream.tile([P, 2 * M], F32, name="o_t", tag="m", align_bytes=64)
            pair = [bank(base + mh * 2 + nt, [P, 512]) for nt in range(2)]
            if i == 0 or (i == 1 and mh == 0):
                for g in range(G):
                    for nt in range(2):
                        pass_t(i, pair[nt], mh, nt, g)
                for nt in range(2):
                    out_t(i, pair[nt], mh, nt)
            else:
                for nt in range(2):
                    for g in range(G):
                        pass_t(i, pair[nt], mh, nt, g)
                    out_t(i, pair[nt], mh, nt)
                    if i < N_FIRST and (mh, nt) != (1, 1):
                        sign_some(1)

        ots = {}

        def finish_t(i, half):
            base = ((i + 1) % 2) * 4
            if half == 0:
                ots[i] = stream.tile([P, 8 * ROWS], F32, name="ot", tag="w", bufs=4)
            ot = ots[i]
            cols = slice(i * ROWS, (i + 1) * ROWS)
            for q in (2 * half, 2 * half + 1):
                bt = bank(base + q, [P, 2 * ROWS])
                for h in range(2):
                    for nt in range(2):
                        mo = nt * M + (2 * q + h) * P
                        nc.tensor.transpose(bt[:, h * ROWS + nt * P:h * ROWS + (nt + 1) * P], o_t[i][:, mo:mo + P], ident[:])
                nc.scalar.copy(
                    out=ot[:, q * 2 * ROWS:(q + 1) * 2 * ROWS].rearrange("p (h j r) -> p h j r", h=2, r=2),
                    in_=bt[:].rearrange("p (h r j) -> p h j r", h=2, r=2),
                )
                if q % 2 == 1:
                    nc.sync.dma_start(
                        out=o_view[:, (q - 1) * 2:(q + 1) * 2, cols],
                        in_=ot[:, (q - 1) * 2 * ROWS:(q + 1) * 2 * ROWS].rearrange("p (i n) -> p i n", i=4),
                    )

        def multiply_n(i, half):
            accs.setdefault(i, {})
            for q in (2 * half, 2 * half + 1):
                acc = bank(((i + 1) % 2) * 4 + q, [P, 2 * ROWS])
                for h in range(2):
                    for g in range(G):
                        lo = g * M + (2 * q + h) * P
                        nc.tensor.matmul_mx(
                            out=acc[:, h * ROWS:(h + 1) * ROWS],
                            lhsT=xc[:, lo:lo + P].bitcast(FP8X4), lhsT_scale=xs[:, lo:lo + P],
                            rhs=wc[i][:, g * ROWS:(g + 1) * ROWS].bitcast(FP8X4), rhs_scale=ws[i][:, g * ROWS:(g + 1) * ROWS],
                            start=(g == 0), stop=(g == G - 1),
                        )
                accs[i][q] = acc

        def finish_n(i, half):
            if half == 0:
                ots[i] = stream.tile([P, 8 * ROWS], F32, name="ot", tag="w", bufs=4)
            ot = ots[i]
            cols = slice(i * ROWS, (i + 1) * ROWS)
            bcols = slice((i - N_FIRST) * ROWS, (i - N_FIRST + 1) * ROWS)
            for q in (2 * half, 2 * half + 1):
                nc.vector.tensor_tensor(
                    out=ot[:, q * 2 * ROWS:(q + 1) * 2 * ROWS].rearrange("p (h j r) -> p h j r", h=2, r=2),
                    in0=accs[i][q][:].rearrange("p (h r j) -> p h j r", h=2, r=2),
                    in1=bias_bc[:, bcols].rearrange("p (j r) -> p j r", r=2).unsqueeze(1).to_broadcast([P, 2, P, 2]),
                    op=ALU.add,
                )
                nc.sync.dma_start(
                    out=o_view[:, q * 2:(q + 1) * 2, cols],
                    in_=ot[:, q * 2 * ROWS:(q + 1) * 2 * ROWS].rearrange("p (i n) -> p i n", i=2),
                )

        Q = PIECE // G
        transpose_row(xts[0][:], xgs[0][:], 0, 0, SS)
        transpose_row(xts[0][:], xgs[0][:], 1, 2, SS)
        transpose_x(1)
        codes(0)
        tern_abs(0, 0, PIECE // 2)
        tern_abs(0, PIECE // 2, PIECE)
        tern_sign(0, 0, PIECE // 2)
        tern_sign(0, PIECE // 2, PIECE)
        quantise_x(0, range(G))
        quantise_w(0, 0, PIECE)
        transpose_x(2)
        transpose_x(3)
        quantise_x(1, range(G))
        sign_some(0)
        multiply_t(0, 0)
        sign_some(2)
        quantise_x(2, range(G))
        tern_abs(1, 0, PIECE)
        quantise_x(3, range(G))
        codes(1)
        tern_sign(1, 0, HALF)
        tern_sign(1, HALF, PIECE)
        quantise_w(1, 0, HALF)
        quantise_w(1, HALF, PIECE)
        tern_abs(2, 0, HALF)
        tern_abs(2, HALF, PIECE)
        multiply_t(0, 1)
        sign_some(2)
        multiply_t(1, 0)
        finish_t(0, 0)
        multiply_t(1, 1)
        finish_t(0, 1)
        for i in range(2, PIECES):
            if i == 2:
                absolute_row(a, 1)
            tern_sign(i, 0, HALF)
            tern_sign(i, HALF, PIECE)
            codes(i)
            if i + 1 < PIECES:
                tern_abs(i + 1, 0, HALF)
                quantise_w(i, 0, PIECE)
                tern_abs(i + 1, HALF, PIECE)
            else:
                quantise_w(i, 0, HALF)
                quantise_w(i, HALF, PIECE)
            for half in range(2):
                if not is_t(i - 2, half):
                    finish_n(i - 2, half)
            for half in range(2):
                if is_t(i, half):
                    multiply_t(i, half)
                else:
                    multiply_n(i, half)
                if is_t(i - 1, half):
                    finish_t(i - 1, half)
            if i == N_FIRST:
                sign_some(len(sign_queue))
        for i in (PIECES - 2, PIECES - 1):
            for half in range(2):
                finish_n(i, half)
